import numpy as np
import ml_dtypes


def mxq(x, axis, fmt="e4m3"):
    dtype, down = {"e4m3": (ml_dtypes.float8_e4m3fn, 7), "e5m2": (ml_dtypes.float8_e5m2, 14)}[fmt]
    v = np.moveaxis(np.asarray(x, np.float32).astype(ml_dtypes.bfloat16).astype(np.float64), axis, -1)
    blocks = v.reshape(v.shape[:-1] + (-1, 32))
    amax = np.abs(blocks).max(-1, keepdims=True)
    byte = np.maximum(np.where(amax > 0, np.frexp(amax)[1] - 1 + 127, 0) - down, 1)
    scale = np.exp2(byte - 127.0)
    codes = (blocks / scale).astype(np.float32).astype(dtype).astype(np.float64)
    return np.moveaxis((codes * scale).reshape(v.shape), -1, axis)


WIDE = False


def mx_kscale(k):
    if not WIDE:
        return np.ones(k)
    levels = np.array([10, -10, 5, -5, 0])
    a = np.random.permutation(np.resize(levels, k // 512 * 4)).reshape(k // 512, 4)
    idx = np.arange(k)
    return np.exp2(a[idx // 512, idx % 128 // 32])


BF16 = ml_dtypes.bfloat16


def bf(x):
    return np.asarray(x, np.float32).astype(BF16)


def f64(x):
    return np.asarray(x).astype(np.float64)


B, C, H, W, R, G, K = 1, 16384, 16, 8, 512, 128, 7
PAD = K // 2
KK = K * K


def setup_inputs():
    t = mx_kscale(R)
    return {"x": bf(np.random.standard_normal((B, C, H, W))),
            "w_reduce": bf(np.random.standard_normal((R, C)) * 1.0 / np.sqrt(C) * t[:, None]),
            "b_reduce": bf(np.random.standard_normal(R) * 0.5 * t),
            "w_span": bf(np.random.standard_normal((KK * G, R)) * 1.5 / np.sqrt(R) / t[None, :]),
            "b_span": bf(np.random.standard_normal(KK * G) * 0.5)}


def reference(x, w_reduce, b_reduce, w_span, b_span):
    x = f64(x)
    red = np.maximum((mxq(f64(w_reduce), 1, "e4m3") @ mxq(x.reshape(B, C, H * W), 1, "e4m3")) + f64(b_reduce)[None, :, None], 0.0)
    kern = (mxq(f64(w_span), 1, "e4m3") @ mxq(red, 1, "e4m3")) + f64(b_span)[None, :, None]
    kern = kern.reshape(B, G, KK, H, W)
    e = np.exp(kern - kern.max(axis=2, keepdims=True))
    kern = e / e.sum(axis=2, keepdims=True)
    xp = np.pad(x, ((0, 0), (0, 0), (PAD, PAD), (PAD, PAD)))
    xg = xp.reshape(B, G, C // G, H + 2 * PAD, W + 2 * PAD)
    out = np.zeros((B, G, C // G, H, W))
    for i in range(K):
        for j in range(K):
            out = out + kern[:, :, None, i * K + j] * xg[:, :, :, i:i + H, j:j + W]
    return out.reshape(B, C, H, W)

@@ -1,0 +1,223 @@
+import concourse.mybir as mybir
+from concourse.masks import make_identity
+
+F32 = mybir.dt.float32
+BF16 = mybir.dt.bfloat16
+U32 = mybir.dt.uint32
+U8 = mybir.dt.uint8
+FP8X4 = mybir.dt.float8_e4m3fn_x4
+ALU = mybir.AluOpType
+ACT = mybir.ActivationFunctionType
+AXIS = mybir.AxisListType
+
+P = 128
+C, H, W, R, G, KS = 16384, 16, 8, 512, 128, 7
+PIX = H * W
+CH = C // G
+TAPS = KS * KS
+PAD = KS // 2
+K_PASS = 4 * P
+PASSES = C // K_PASS
+CHUNK_PASSES = 8
+CHUNKS = PASSES // CHUNK_PASSES
+R_BLOCKS = R // P
+SPAN_LOAD_TAPS = 7
+ROWS_PER_BLOCK = 4
+X_PIECE = 32
+
+FLOPS = 2 * R * C * PIX + 2 * TAPS * G * R * PIX + 2 * C * PIX * TAPS
+
+
+def tile_involution_k_kernel(tc, x, w_reduce, b_reduce, w_span, b_span, out):
+    nc = tc.nc
+    x_rows = x.rearrange("b c h w -> (b c) (h w)")
+    x_by_pass = x_rows.rearrange("(q u p e) s -> p q u (e s)", q=PASSES, u=2, p=P, e=2)
+    x_by_group = x_rows.rearrange("(g c) s -> g c s", c=CH)
+    out_by_group = out.rearrange("b (g c) h w -> g c (b h w)", c=CH)
+    w_blocks = w_reduce.rearrange("(u p e) c -> u e p c", u=2, p=P, e=2)
+    span_by_group = w_span.rearrange("(g t) r -> g t r", t=TAPS)
+
+    with tc.tile_pool(name="const", bufs=1) as const, tc.tile_pool(name="keep", bufs=1) as keep:
+        ident = const.tile([P, P], F32)
+        make_identity(nc, ident[:])
+        x_t = keep.tile([P, PIX, CH], BF16)
+        prob = keep.tile([P, TAPS, PIX], F32)
+        top = keep.tile([P, PIX], F32)
+        total = keep.tile([P, PIX], F32)
+
+        b_red_bf = const.tile([P, R_BLOCKS], BF16)
+        nc.scalar.dma_start(
+            out=b_red_bf[:].rearrange("p (u e) -> p u e", u=2), in_=b_reduce.rearrange("(u p e) -> p u e", u=2, p=P, e=2)
+        )
+        b_red = const.tile([P, R_BLOCKS], F32)
+        nc.vector.tensor_copy(out=b_red[:], in_=b_red_bf[:])
+        b_tap_bf = const.tile([P, TAPS], BF16)
+        nc.scalar.dma_start(out=b_tap_bf[:], in_=b_span.rearrange("(g t) -> g t", t=TAPS))
+        b_tap = const.tile([P, TAPS], F32)
+        nc.vector.tensor_copy(out=b_tap[:], in_=b_tap_bf[:])
+
+        with tc.tile_pool(name="codes", bufs=1) as codes, tc.tile_pool(name="xstage", bufs=2) as xstage, tc.tile_pool(
+            name="wload", bufs=3
+        ) as wload, tc.tile_pool(name="wstage", bufs=2) as wstage, tc.tile_pool(name="sload", bufs=2) as sload, tc.tile_pool(
+            name="sstage", bufs=3
+        ) as sstage, tc.tile_pool(name="xgload", bufs=2) as xgload, tc.psum_pool(name="flip", bufs=4) as flip, tc.psum_pool(
+            name="sums", bufs=4
+        ) as sums:
+            x_codes = codes.tile([P, PASSES * PIX], U32, align_bytes=64)
+            x_scales = codes.tile([P, PASSES * PIX], U8, align_bytes=64)
+            for chunk in range(CHUNKS):
+                x_raw = xstage.tile([P, CHUNK_PASSES, 4, PIX], BF16)
+                nc.sync.dma_start(
+                    out=x_raw[:].rearrange("p q (u e) s -> p q u (e s)", u=2),
+                    in_=x_by_pass[:, chunk * CHUNK_PASSES : (chunk + 1) * CHUNK_PASSES],
+                )
+                x_grouped = xstage.tile([P, CHUNK_PASSES, PIX, 4], BF16, align_bytes=64)
+                nc.vector.tensor_copy(out=x_grouped[:], in_=x_raw[:].rearrange("p q t s -> p q s t"))
+                cols = slice(chunk * CHUNK_PASSES * PIX, (chunk + 1) * CHUNK_PASSES * PIX)
+                nc.vector.quantize_mx(
+                    out=x_codes[:, cols].bitcast(FP8X4),
+                    scales=x_scales[:, cols],
+                    in_=x_grouped[:].rearrange("p q s t -> p (q s t)"),
+                )
+
+            span_codes = codes.tile([P, TAPS, G], U32, align_bytes=64)
+            span_scales = codes.tile([P, TAPS, G], U8, align_bytes=64)
+            for load in range(TAPS // SPAN_LOAD_TAPS):
+                span_raw = sload.tile([P, SPAN_LOAD_TAPS, R], BF16)
+                nc.sync.dma_start(
+                    out=span_raw[:], in_=span_by_group[:, load * SPAN_LOAD_TAPS : (load + 1) * SPAN_LOAD_TAPS, :]
+                )
+                for k in range(SPAN_LOAD_TAPS):
+                    tap = load * SPAN_LOAD_TAPS + k
+                    span_words = span_raw[:, k, :].bitcast(F32)
+                    span_flip = flip.tile([P, 2, G], F32, tag="flip")
+                    for u in range(2):
+                        nc.tensor.transpose(span_flip[:, u, :], span_words[:, u * P : (u + 1) * P], ident[:])
+                    span_grouped = sstage.tile([P, G, 2], F32, align_bytes=64)
+                    nc.scalar.copy(out=span_grouped[:], in_=span_flip[:].rearrange("p u g -> p g u"))
+                    nc.vector.quantize_mx(
+                        out=span_codes[:, tap, :].bitcast(FP8X4),
+                        scales=span_scales[:, tap, :],
+                        in_=span_grouped[:].rearrange("p g u -> p (g u)").bitcast(BF16),
+                    )
+
+            red_sums = [sums.tile([P, PIX], F32, name="red_sums%d" % blk, tag="sums") for blk in range(R_BLOCKS)]
+            for chunk in range(CHUNKS):
+                for blk in range(R_BLOCKS):
+                    w_raw = wload.tile([P, CHUNK_PASSES * K_PASS], BF16)
+                    nc.sync.dma_start(
+                        out=w_raw[:],
+                        in_=w_blocks[
+                            blk // 2, blk % 2, :, chunk * CHUNK_PASSES * K_PASS : (chunk + 1) * CHUNK_PASSES * K_PASS
+                        ],
+                    )
+                    w_words = w_raw[:].bitcast(F32)
+                    w_grouped = wstage.tile([P, CHUNK_PASSES, P, 2], F32, align_bytes=64)
+                    for pair in range(CHUNK_PASSES // 2):
+                        w_flip = flip.tile([P, 2, 2, P], F32, tag="flip")
+                        for q in range(2):
+                            for u in range(2):
+                                first = (2 * pair + q) * 2 * P + u * P
+                                nc.tensor.transpose(w_flip[:, q, u, :], w_words[:, first : first + P], ident[:])
+                        copy_out = nc.scalar.copy if pair % 2 == 0 else nc.vector.tensor_copy
+                        copy_out(
+                            out=w_grouped[:, 2 * pair : 2 * pair + 2, :, :], in_=w_flip[:].rearrange("p q u r -> p q r u")
+                        )
+                    w_codes = wstage.tile([P, CHUNK_PASSES * P], U32, align_bytes=64)
+                    w_scales = wstage.tile([P, CHUNK_PASSES * P], U8, align_bytes=64)
+                    nc.vector.quantize_mx(
+                        out=w_codes[:].bitcast(FP8X4),
+                        scales=w_scales[:],
+                        in_=w_grouped[:].rearrange("p q r u -> p (q r u)").bitcast(BF16),
+                    )
+                    for q in range(CHUNK_PASSES):
+                        k_pass = chunk * CHUNK_PASSES + q
+                        nc.tensor.matmul_mx(
+                            out=red_sums[blk][:],
+                            lhsT=w_codes[:, q * P : (q + 1) * P].bitcast(FP8X4),
+                            lhsT_scale=w_scales[:, q * P : (q + 1) * P],
+                            rhs=x_codes[:, k_pass * PIX : (k_pass + 1) * PIX].bitcast(FP8X4),
+                            rhs_scale=x_scales[:, k_pass * PIX : (k_pass + 1) * PIX],
+                            start=(k_pass == 0),
+                            stop=(k_pass == PASSES - 1),
+                        )
+
+            red_grouped = codes.tile([P, PIX, R_BLOCKS], BF16, align_bytes=64)
+            for blk in range(R_BLOCKS):
+                nc.scalar.activation(
+                    out=red_grouped[:, :, blk], in_=red_sums[blk][:], func=ACT.Relu, bias=b_red[:, blk : blk + 1], scale=1.0
+                )
+            red_codes = codes.tile([P, PIX], U32, align_bytes=64)
+            red_scales = codes.tile([P, PIX], U8, align_bytes=64)
+            nc.vector.quantize_mx(
+                out=red_codes[:].bitcast(FP8X4), scales=red_scales[:], in_=red_grouped[:].rearrange("p s t -> p (s t)")
+            )
+
+            for first_tap in range(0, TAPS, 4):
+                n_taps = min(4, TAPS - first_tap)
+                kern_sums = sums.tile([P, 4, PIX], F32, tag="sums")
+                for k in range(n_taps):
+                    nc.tensor.matmul_mx(
+                        out=kern_sums[:, k, :],
+                        lhsT=span_codes[:, first_tap + k, :].bitcast(FP8X4),
+                        lhsT_scale=span_scales[:, first_tap + k, :],
+                        rhs=red_codes[:].bitcast(FP8X4),
+                        rhs_scale=red_scales[:],
+                        start=True,
+                        stop=True,
+                    )
+                nc.vector.tensor_tensor(
+                    out=prob[:, first_tap : first_tap + n_taps, :],
+                    in0=kern_sums[:, 0:n_taps, :],
+                    in1=b_tap[:, first_tap : first_tap + n_taps].unsqueeze(2).to_broadcast([P, n_taps, PIX]),
+                    op=ALU.add,
+                )
+
+            for piece in range(CH // X_PIECE):
+                chans = slice(piece * X_PIECE, (piece + 1) * X_PIECE)
+                x_group = xgload.tile([P, X_PIECE, PIX], BF16)
+                nc.sync.dma_start(out=x_group[:], in_=x_by_group[:, chans, :])
+                nc.scalar.copy(out=x_t[:, :, chans], in_=x_group[:].rearrange("p c s -> p s c"))
+
+        nc.vector.tensor_reduce(out=top[:], in_=prob[:].rearrange("p t s -> p s t"), axis=AXIS.X, op=ALU.max)
+        nc.vector.tensor_tensor(
+            out=prob[:], in0=prob[:], in1=top[:].unsqueeze(1).to_broadcast([P, TAPS, PIX]), op=ALU.subtract
+        )
+        nc.scalar.activation(out=prob[:], in_=prob[:], func=ACT.Exp)
+        nc.vector.tensor_reduce(out=total[:], in_=prob[:].rearrange("p t s -> p s t"), axis=AXIS.X, op=ALU.add)
+        nc.vector.reciprocal(out=total[:], in_=total[:])
+        nc.vector.tensor_tensor(
+            out=prob[:], in0=prob[:], in1=total[:].unsqueeze(1).to_broadcast([P, TAPS, PIX]), op=ALU.mult
+        )
+
+        centre = PAD * KS + PAD
+        block_pix = ROWS_PER_BLOCK * W
+        with tc.tile_pool(name="acc", bufs=2) as accs, tc.tile_pool(name="res", bufs=2) as ress:
+            for block in range(H // ROWS_PER_BLOCK):
+                rows = range(block * ROWS_PER_BLOCK, (block + 1) * ROWS_PER_BLOCK)
+                acc = accs.tile([P, block_pix, CH], F32)
+                for pix in range(block * block_pix, (block + 1) * block_pix):
+                    nc.vector.tensor_scalar_mul(
+                        out=acc[:, pix - block * block_pix, :], in0=x_t[:, pix, :], scalar1=prob[:, centre, pix : pix + 1]
+                    )
+                for tap in range(TAPS):
+                    if tap == centre:
+                        continue
+                    dh, dw = tap // KS - PAD, tap % KS - PAD
+                    for h in rows:
+                        for w in range(W):
+                            if not (0 <= h + dh < H and 0 <= w + dw < W):
+                                continue
+                            pix = h * W + w
+                            mine = acc[:, pix - block * block_pix, :]
+                            nc.vector.scalar_tensor_tensor(
+                                out=mine,
+                                in0=x_t[:, (h + dh) * W + w + dw, :],
+                                scalar=prob[:, tap, pix : pix + 1],
+                                in1=mine,
+                                op0=ALU.mult,
+                                op1=ALU.add,
+                            )
+                res = ress.tile([P, CH, block_pix], F32)
+                nc.scalar.copy(out=res[:], in_=acc[:].rearrange("p s c -> p c s"))
+                nc.sync.dma_start(out=out_by_group[:, :, block * block_pix : (block + 1) * block_pix], in_=res[:])

@@ -24,6 +24,13 @@ R_BLOCKS = R // P
 SPAN_LOAD_TAPS = 7
 ROWS_PER_BLOCK = 4
 X_PIECE = 32
+EDGE_BLOCKS = (0, 3)
+MID_FIRST_ROW, MID_ROWS = 4, 8
+MID_PIX = MID_ROWS * W
+SLOT_PITCH = W
+SLOTS = KS * SLOT_PITCH
+CENTRE_SLOT = PAD * SLOT_PITCH + PAD
+GROUPS_PER_ROUND = 8
 
 FLOPS = 2 * R * C * PIX + 2 * TAPS * G * R * PIX + 2 * C * PIX * TAPS
 
@@ -34,12 +41,30 @@ def tile_involution_k_kernel(tc, x, w_reduce, b_reduce, w_span, b_span, out):
     x_by_pass = x_rows.rearrange("(q u p e) s -> p q u (e s)", q=PASSES, u=2, p=P, e=2)
     x_by_group = x_rows.rearrange("(g c) s -> g c s", c=CH)
     out_by_group = out.rearrange("b (g c) h w -> g c (b h w)", c=CH)
+    x_by_channel = x_rows.rearrange("(g c) s -> c g s", c=CH)
+    out_by_channel = out.rearrange("b (g c) h w -> c g (b h w)", c=CH)
+    out_rows = out.rearrange("b c h w -> (b c) (h w)")
     w_blocks = w_reduce.rearrange("(u p e) c -> u e p c", u=2, p=P, e=2)
     span_by_group = w_span.rearrange("(g t) r -> g t r", t=TAPS)
 
     with tc.tile_pool(name="const", bufs=1) as const, tc.tile_pool(name="keep", bufs=1) as keep:
         ident = const.tile([P, P], F32)
         make_identity(nc, ident[:])
+        ident_bf = const.tile([P, P], BF16)
+        make_identity(nc, ident_bf[:])
+
+        ident_hw = ident[:].rearrange("p (h w) -> p h w", w=W)
+        same_row = const.tile([P, H, W], F32)
+        nc.vector.tensor_copy(out=same_row[:], in_=ident_hw)
+        for dw in range(1, PAD + 1):
+            nc.vector.tensor_add(out=same_row[:, :, 0 : W - dw], in0=same_row[:, :, 0 : W - dw], in1=ident_hw[:, :, dw:W])
+            nc.vector.tensor_add(out=same_row[:, :, dw:W], in0=same_row[:, :, dw:W], in1=ident_hw[:, :, 0 : W - dw])
+        in_window = const.tile([P, MID_ROWS, W], F32)
+        nc.vector.tensor_copy(out=in_window[:], in_=same_row[:, MID_FIRST_ROW : MID_FIRST_ROW + MID_ROWS, :])
+        for dh in range(1, PAD + 1):
+            for first in (MID_FIRST_ROW + dh, MID_FIRST_ROW - dh):
+                nc.vector.tensor_add(out=in_window[:], in0=in_window[:], in1=same_row[:, first : first + MID_ROWS, :])
+        in_window_cols = in_window[:].rearrange("p h w -> p (h w)")
         x_t = keep.tile([P, PIX, CH], BF16)
         prob = keep.tile([P, TAPS, PIX], F32)
         top = keep.tile([P, PIX], F32)
@@ -190,10 +215,56 @@ def tile_involution_k_kernel(tc, x, w_reduce, b_reduce, w_span, b_span, out):
             out=prob[:], in0=prob[:], in1=total[:].unsqueeze(1).to_broadcast([P, TAPS, PIX]), op=ALU.mult
         )
 
-        centre = PAD * KS + PAD
-        block_pix = ROWS_PER_BLOCK * W
-        with tc.tile_pool(name="acc", bufs=2) as accs, tc.tile_pool(name="res", bufs=2) as ress:
-            for block in range(H // ROWS_PER_BLOCK):
+        with tc.tile_pool(name="band", bufs=1) as bands, tc.tile_pool(name="mid", bufs=2) as mid, tc.psum_pool(
+            name="pflip", bufs=2
+        ) as pflip, tc.psum_pool(name="xflip", bufs=2) as xflip, tc.psum_pool(name="osum", bufs=2) as osum, tc.tile_pool(
+            name="acc", bufs=2
+        ) as accs, tc.tile_pool(name="res", bufs=2) as ress:
+            by_pixel = bands.tile([P, KS, SLOT_PITCH, G], F32, tag="wide")
+            nc.vector.memset(by_pixel[:, :, KS, :], 0.0)
+            for i in range(KS):
+                for first_j in range(0, KS, 4):
+                    n_taps = min(4, KS - first_j)
+                    prob_flip = pflip.tile([P, 4, G], F32)
+                    for k in range(n_taps):
+                        nc.tensor.transpose(prob_flip[:, k, :], prob[:, i * KS + first_j + k, :], ident[:])
+                    nc.scalar.copy(out=by_pixel[:, i, first_j : first_j + n_taps, :], in_=prob_flip[:, 0:n_taps, :])
+            nc.sync.dma_start(
+                out=out_rows[0 : PIX * SLOTS, :].rearrange("(s k) g -> s (k g)", k=SLOTS),
+                in_=by_pixel[:].rearrange("p i j g -> p (i j g)"),
+            )
+            by_source = bands.tile([P, MID_PIX, G], F32)
+            for k in range(MID_PIX):
+                first = (SLOTS - 1) * (MID_FIRST_ROW * W + k) + CENTRE_SLOT
+                nc.sync.dma_start(out=by_source[:, k, :], in_=out_rows[first : first + PIX, :])
+            band = bands.tile([P, G, MID_PIX], F32, tag="wide")
+            for k in range(MID_PIX):
+                nc.scalar.activation(
+                    out=band[:, :, k], in_=by_source[:, k, :], func=ACT.Copy, scale=in_window_cols[:, k : k + 1]
+                )
+            for first_g in range(0, G, GROUPS_PER_ROUND):
+                groups = slice(first_g, first_g + GROUPS_PER_ROUND)
+                x_chan = mid.tile([P, GROUPS_PER_ROUND, PIX], BF16)
+                nc.sync.dma_start(out=x_chan[:], in_=x_by_channel[:, groups, :])
+                x_flip = xflip.tile([P, GROUPS_PER_ROUND, CH], BF16)
+                for k in range(GROUPS_PER_ROUND):
+                    nc.tensor.transpose(x_flip[:, k, :], x_chan[:, k, :], ident_bf[:])
+                x_source = mid.tile([P, GROUPS_PER_ROUND, CH], F32)
+                nc.scalar.copy(out=x_source[:], in_=x_flip[:])
+                mid_sums = osum.tile([P, GROUPS_PER_ROUND, MID_PIX], F32)
+                for k in range(GROUPS_PER_ROUND):
+                    nc.tensor.matmul(
+                        out=mid_sums[:, k, :], lhsT=x_source[:, k, :], rhs=band[:, first_g + k, :], start=True, stop=True
+                    )
+                mid_res = mid.tile([P, GROUPS_PER_ROUND, MID_PIX], F32)
+                nc.scalar.copy(out=mid_res[:], in_=mid_sums[:])
+                nc.sync.dma_start(
+                    out=out_by_channel[:, groups, MID_FIRST_ROW * W : MID_FIRST_ROW * W + MID_PIX], in_=mid_res[:]
+                )
+
+            centre = PAD * KS + PAD
+            block_pix = ROWS_PER_BLOCK * W
+            for block in EDGE_BLOCKS:
                 rows = range(block * ROWS_PER_BLOCK, (block + 1) * ROWS_PER_BLOCK)
                 acc = accs.tile([P, block_pix, CH], F32)
                 for pix in range(block * block_pix, (block + 1) * block_pix):

@@ -20,10 +20,12 @@ K_PASS = 4 * P
 PASSES = C // K_PASS
 CHUNK_PASSES = 8
 CHUNKS = PASSES // CHUNK_PASSES
+X_CHUNK_PASSES = 4
 R_BLOCKS = R // P
 SPAN_LOAD_TAPS = 7
 ROWS_PER_BLOCK = 4
-X_PIECE = 32
+X_LOAD_GROUPS = 32
+RES_CHANNELS = 32
 EDGE_BLOCKS = (0, 3)
 MID_FIRST_ROW, MID_ROWS = 4, 8
 MID_PIX = MID_ROWS * W
@@ -39,7 +41,6 @@ def tile_involution_k_kernel(tc, x, w_reduce, b_reduce, w_span, b_span, out):
     nc = tc.nc
     x_rows = x.rearrange("b c h w -> (b c) (h w)")
     x_by_pass = x_rows.rearrange("(q u p e) s -> p q u (e s)", q=PASSES, u=2, p=P, e=2)
-    x_by_group = x_rows.rearrange("(g c) s -> g c s", c=CH)
     out_by_group = out.rearrange("b (g c) h w -> g c (b h w)", c=CH)
     x_by_channel = x_rows.rearrange("(g c) s -> c g s", c=CH)
     out_by_channel = out.rearrange("b (g c) h w -> c g (b h w)", c=CH)
@@ -65,6 +66,7 @@ def tile_involution_k_kernel(tc, x, w_reduce, b_reduce, w_span, b_span, out):
             for first in (MID_FIRST_ROW + dh, MID_FIRST_ROW - dh):
                 nc.vector.tensor_add(out=in_window[:], in0=in_window[:], in1=same_row[:, first : first + MID_ROWS, :])
         in_window_cols = in_window[:].rearrange("p h w -> p (h w)")
+        x_chan = keep.tile([P, G, PIX], BF16)
         x_t = keep.tile([P, PIX, CH], BF16)
         prob = keep.tile([P, TAPS, PIX], F32)
         top = keep.tile([P, PIX], F32)
@@ -85,26 +87,7 @@ def tile_involution_k_kernel(tc, x, w_reduce, b_reduce, w_span, b_span, out):
             name="wload", bufs=3
         ) as wload, tc.tile_pool(name="wstage", bufs=2) as wstage, tc.tile_pool(name="sload", bufs=2) as sload, tc.tile_pool(
             name="sstage", bufs=3
-        ) as sstage, tc.tile_pool(name="xgload", bufs=2) as xgload, tc.psum_pool(name="flip", bufs=4) as flip, tc.psum_pool(
-            name="sums", bufs=4
-        ) as sums:
-            x_codes = codes.tile([P, PASSES * PIX], U32, align_bytes=64)
-            x_scales = codes.tile([P, PASSES * PIX], U8, align_bytes=64)
-            for chunk in range(CHUNKS):
-                x_raw = xstage.tile([P, CHUNK_PASSES, 4, PIX], BF16)
-                nc.sync.dma_start(
-                    out=x_raw[:].rearrange("p q (u e) s -> p q u (e s)", u=2),
-                    in_=x_by_pass[:, chunk * CHUNK_PASSES : (chunk + 1) * CHUNK_PASSES],
-                )
-                x_grouped = xstage.tile([P, CHUNK_PASSES, PIX, 4], BF16, align_bytes=64)
-                nc.vector.tensor_copy(out=x_grouped[:], in_=x_raw[:].rearrange("p q t s -> p q s t"))
-                cols = slice(chunk * CHUNK_PASSES * PIX, (chunk + 1) * CHUNK_PASSES * PIX)
-                nc.vector.quantize_mx(
-                    out=x_codes[:, cols].bitcast(FP8X4),
-                    scales=x_scales[:, cols],
-                    in_=x_grouped[:].rearrange("p q s t -> p (q s t)"),
-                )
-
+        ) as sstage, tc.psum_pool(name="flip", bufs=4) as flip, tc.psum_pool(name="sums", bufs=4) as sums:
             span_codes = codes.tile([P, TAPS, G], U32, align_bytes=64)
             span_scales = codes.tile([P, TAPS, G], U8, align_bytes=64)
             for load in range(TAPS // SPAN_LOAD_TAPS):
@@ -126,6 +109,23 @@ def tile_involution_k_kernel(tc, x, w_reduce, b_reduce, w_span, b_span, out):
                         in_=span_grouped[:].rearrange("p g u -> p (g u)").bitcast(BF16),
                     )
 
+            x_codes = codes.tile([P, PASSES * PIX], U32, align_bytes=64)
+            x_scales = codes.tile([P, PASSES * PIX], U8, align_bytes=64)
+            for chunk in range(PASSES // X_CHUNK_PASSES):
+                x_raw = xstage.tile([P, X_CHUNK_PASSES, 4, PIX], BF16)
+                nc.sync.dma_start(
+                    out=x_raw[:].rearrange("p q (u e) s -> p q u (e s)", u=2),
+                    in_=x_by_pass[:, chunk * X_CHUNK_PASSES : (chunk + 1) * X_CHUNK_PASSES],
+                )
+                x_grouped = xstage.tile([P, X_CHUNK_PASSES, PIX, 4], BF16, align_bytes=64)
+                nc.vector.tensor_copy(out=x_grouped[:], in_=x_raw[:].rearrange("p q t s -> p q s t"))
+                cols = slice(chunk * X_CHUNK_PASSES * PIX, (chunk + 1) * X_CHUNK_PASSES * PIX)
+                nc.vector.quantize_mx(
+                    out=x_codes[:, cols].bitcast(FP8X4),
+                    scales=x_scales[:, cols],
+                    in_=x_grouped[:].rearrange("p q s t -> p (q s t)"),
+                )
+
             red_sums = [sums.tile([P, PIX], F32, name="red_sums%d" % blk, tag="sums") for blk in range(R_BLOCKS)]
             for chunk in range(CHUNKS):
                 for blk in range(R_BLOCKS):
@@ -144,7 +144,7 @@ def tile_involution_k_kernel(tc, x, w_reduce, b_reduce, w_span, b_span, out):
                             for u in range(2):
                                 first = (2 * pair + q) * 2 * P + u * P
                                 nc.tensor.transpose(w_flip[:, q, u, :], w_words[:, first : first + P], ident[:])
-                        copy_out = nc.scalar.copy if pair % 2 == 0 else nc.vector.tensor_copy
+                        copy_out = nc.vector.tensor_copy if pair == 0 else nc.scalar.copy
                         copy_out(
                             out=w_grouped[:, 2 * pair : 2 * pair + 2, :, :], in_=w_flip[:].rearrange("p q u r -> p q r u")
                         )
@@ -198,28 +198,39 @@ def tile_involution_k_kernel(tc, x, w_reduce, b_reduce, w_span, b_span, out):
                     op=ALU.add,
                 )
 
-            for piece in range(CH // X_PIECE):
-                chans = slice(piece * X_PIECE, (piece + 1) * X_PIECE)
-                x_group = xgload.tile([P, X_PIECE, PIX], BF16)
-                nc.sync.dma_start(out=x_group[:], in_=x_by_group[:, chans, :])
-                nc.scalar.copy(out=x_t[:, :, chans], in_=x_group[:].rearrange("p c s -> p s c"))
+            for first_g in range(0, G, X_LOAD_GROUPS):
+                groups = slice(first_g, first_g + X_LOAD_GROUPS)
+                nc.sync.dma_start(out=x_chan[:, groups, :], in_=x_by_channel[:, groups, :])
+            for row in range(H):
+                if MID_FIRST_ROW + PAD <= row < MID_FIRST_ROW + MID_ROWS - PAD:
+                    continue
+                x_row_flip = flip.tile([P, W, CH], BF16, tag="flip")
+                for w in range(W):
+                    nc.tensor.transpose(x_row_flip[:, w, :], x_chan[:, :, row * W + w], ident_bf[:])
+                nc.scalar.copy(out=x_t[:, row * W : (row + 1) * W, :], in_=x_row_flip[:])
 
-        nc.vector.tensor_reduce(out=top[:], in_=prob[:].rearrange("p t s -> p s t"), axis=AXIS.X, op=ALU.max)
-        nc.vector.tensor_tensor(
-            out=prob[:], in0=prob[:], in1=top[:].unsqueeze(1).to_broadcast([P, TAPS, PIX]), op=ALU.subtract
-        )
-        nc.scalar.activation(out=prob[:], in_=prob[:], func=ACT.Exp)
-        nc.vector.tensor_reduce(out=total[:], in_=prob[:].rearrange("p t s -> p s t"), axis=AXIS.X, op=ALU.add)
-        nc.vector.reciprocal(out=total[:], in_=total[:])
-        nc.vector.tensor_tensor(
-            out=prob[:], in0=prob[:], in1=total[:].unsqueeze(1).to_broadcast([P, TAPS, PIX]), op=ALU.mult
-        )
+        block_pix = ROWS_PER_BLOCK * W
+        parts = [(block * block_pix, block_pix) for block in EDGE_BLOCKS] + [(MID_FIRST_ROW * W, MID_PIX)]
+        for first_pix, n_pix in parts:
+            part = slice(first_pix, first_pix + n_pix)
+            logits = prob[:, :, part]
+            by_tap_last = logits.rearrange("p t s -> p s t")
+            nc.vector.tensor_reduce(out=top[:, part], in_=by_tap_last, axis=AXIS.X, op=ALU.max)
+            nc.vector.tensor_tensor(
+                out=logits, in0=logits, in1=top[:, part].unsqueeze(1).to_broadcast([P, TAPS, n_pix]), op=ALU.subtract
+            )
+            nc.scalar.activation(out=logits, in_=logits, func=ACT.Exp)
+            nc.vector.tensor_reduce(out=total[:, part], in_=by_tap_last, axis=AXIS.X, op=ALU.add)
+            nc.vector.reciprocal(out=total[:, part], in_=total[:, part])
+            nc.vector.tensor_tensor(
+                out=logits, in0=logits, in1=total[:, part].unsqueeze(1).to_broadcast([P, TAPS, n_pix]), op=ALU.mult
+            )
 
         with tc.tile_pool(name="band", bufs=1) as bands, tc.tile_pool(name="mid", bufs=2) as mid, tc.psum_pool(
             name="pflip", bufs=2
         ) as pflip, tc.psum_pool(name="xflip", bufs=2) as xflip, tc.psum_pool(name="osum", bufs=2) as osum, tc.tile_pool(
             name="acc", bufs=2
-        ) as accs, tc.tile_pool(name="res", bufs=2) as ress:
+        ) as accs, tc.tile_pool(name="res", bufs=3) as ress:
             by_pixel = bands.tile([P, KS, SLOT_PITCH, G], F32, tag="wide")
             nc.vector.memset(by_pixel[:, :, KS, :], 0.0)
             for i in range(KS):
@@ -244,11 +255,9 @@ def tile_involution_k_kernel(tc, x, w_reduce, b_reduce, w_span, b_span, out):
                 )
             for first_g in range(0, G, GROUPS_PER_ROUND):
                 groups = slice(first_g, first_g + GROUPS_PER_ROUND)
-                x_chan = mid.tile([P, GROUPS_PER_ROUND, PIX], BF16)
-                nc.sync.dma_start(out=x_chan[:], in_=x_by_channel[:, groups, :])
                 x_flip = xflip.tile([P, GROUPS_PER_ROUND, CH], BF16)
                 for k in range(GROUPS_PER_ROUND):
-                    nc.tensor.transpose(x_flip[:, k, :], x_chan[:, k, :], ident_bf[:])
+                    nc.tensor.transpose(x_flip[:, k, :], x_chan[:, first_g + k, :], ident_bf[:])
                 x_source = mid.tile([P, GROUPS_PER_ROUND, CH], F32)
                 nc.scalar.copy(out=x_source[:], in_=x_flip[:])
                 mid_sums = osum.tile([P, GROUPS_PER_ROUND, MID_PIX], F32)
@@ -263,7 +272,6 @@ def tile_involution_k_kernel(tc, x, w_reduce, b_reduce, w_span, b_span, out):
                 )
 
             centre = PAD * KS + PAD
-            block_pix = ROWS_PER_BLOCK * W
             for block in EDGE_BLOCKS:
                 rows = range(block * ROWS_PER_BLOCK, (block + 1) * ROWS_PER_BLOCK)
                 acc = accs.tile([P, block_pix, CH], F32)
@@ -289,6 +297,8 @@ def tile_involution_k_kernel(tc, x, w_reduce, b_reduce, w_span, b_span, out):
                                 op0=ALU.mult,
                                 op1=ALU.add,
                             )
-                res = ress.tile([P, CH, block_pix], F32)
-                nc.scalar.copy(out=res[:], in_=acc[:].rearrange("p s c -> p c s"))
-                nc.sync.dma_start(out=out_by_group[:, :, block * block_pix : (block + 1) * block_pix], in_=res[:])
+                for first_c in range(0, CH, RES_CHANNELS):
+                    chans = slice(first_c, first_c + RES_CHANNELS)
+                    res = ress.tile([P, RES_CHANNELS, block_pix], F32)
+                    nc.scalar.copy(out=res[:], in_=acc[:, :, chans].rearrange("p s c -> p c s"))
+                    nc.sync.dma_start(out=out_by_group[:, chans, block * block_pix : (block + 1) * block_pix], in_=res[:])

@@ -22,9 +22,10 @@ CHUNK_PASSES = 8
 CHUNKS = PASSES // CHUNK_PASSES
 X_CHUNK_PASSES = 4
 R_BLOCKS = R // P
-SPAN_LOAD_TAPS = 7
+SPAN_LOAD_TAPS = 8
+SPAN_QUANT_TAPS = 4
 ROWS_PER_BLOCK = 4
-X_LOAD_GROUPS = 32
+X_PIECE = 32
 RES_CHANNELS = 32
 EDGE_BLOCKS = (0, 3)
 MID_FIRST_ROW, MID_ROWS = 4, 8
@@ -41,6 +42,7 @@ def tile_involution_k_kernel(tc, x, w_reduce, b_reduce, w_span, b_span, out):
     nc = tc.nc
     x_rows = x.rearrange("b c h w -> (b c) (h w)")
     x_by_pass = x_rows.rearrange("(q u p e) s -> p q u (e s)", q=PASSES, u=2, p=P, e=2)
+    x_by_group = x_rows.rearrange("(g c) s -> g c s", c=CH)
     out_by_group = out.rearrange("b (g c) h w -> g c (b h w)", c=CH)
     x_by_channel = x_rows.rearrange("(g c) s -> c g s", c=CH)
     out_by_channel = out.rearrange("b (g c) h w -> c g (b h w)", c=CH)
@@ -66,7 +68,6 @@ def tile_involution_k_kernel(tc, x, w_reduce, b_reduce, w_span, b_span, out):
             for first in (MID_FIRST_ROW + dh, MID_FIRST_ROW - dh):
                 nc.vector.tensor_add(out=in_window[:], in0=in_window[:], in1=same_row[:, first : first + MID_ROWS, :])
         in_window_cols = in_window[:].rearrange("p h w -> p (h w)")
-        x_chan = keep.tile([P, G, PIX], BF16)
         x_t = keep.tile([P, PIX, CH], BF16)
         prob = keep.tile([P, TAPS, PIX], F32)
         top = keep.tile([P, PIX], F32)
@@ -84,29 +85,37 @@ def tile_involution_k_kernel(tc, x, w_reduce, b_reduce, w_span, b_span, out):
         nc.vector.tensor_copy(out=b_tap[:], in_=b_tap_bf[:])
 
         with tc.tile_pool(name="codes", bufs=1) as codes, tc.tile_pool(name="xstage", bufs=2) as xstage, tc.tile_pool(
-            name="wload", bufs=3
+            name="wload", bufs=4
         ) as wload, tc.tile_pool(name="wstage", bufs=2) as wstage, tc.tile_pool(name="sload", bufs=2) as sload, tc.tile_pool(
-            name="sstage", bufs=3
-        ) as sstage, tc.psum_pool(name="flip", bufs=4) as flip, tc.psum_pool(name="sums", bufs=4) as sums:
+            name="sstage", bufs=2
+        ) as sstage, tc.tile_pool(name="xgload", bufs=2) as xgload, tc.psum_pool(name="flip", bufs=4) as flip, tc.psum_pool(
+            name="sums", bufs=4
+        ) as sums:
             span_codes = codes.tile([P, TAPS, G], U32, align_bytes=64)
             span_scales = codes.tile([P, TAPS, G], U8, align_bytes=64)
-            for load in range(TAPS // SPAN_LOAD_TAPS):
+            for first_tap in range(0, TAPS, SPAN_LOAD_TAPS):
+                n_load = min(SPAN_LOAD_TAPS, TAPS - first_tap)
                 span_raw = sload.tile([P, SPAN_LOAD_TAPS, R], BF16)
-                nc.sync.dma_start(
-                    out=span_raw[:], in_=span_by_group[:, load * SPAN_LOAD_TAPS : (load + 1) * SPAN_LOAD_TAPS, :]
-                )
-                for k in range(SPAN_LOAD_TAPS):
-                    tap = load * SPAN_LOAD_TAPS + k
-                    span_words = span_raw[:, k, :].bitcast(F32)
-                    span_flip = flip.tile([P, 2, G], F32, tag="flip")
-                    for u in range(2):
-                        nc.tensor.transpose(span_flip[:, u, :], span_words[:, u * P : (u + 1) * P], ident[:])
-                    span_grouped = sstage.tile([P, G, 2], F32, align_bytes=64)
-                    nc.scalar.copy(out=span_grouped[:], in_=span_flip[:].rearrange("p u g -> p g u"))
+                nc.sync.dma_start(out=span_raw[:, 0:n_load, :], in_=span_by_group[:, first_tap : first_tap + n_load, :])
+                for batch in range(0, n_load, SPAN_QUANT_TAPS):
+                    n_batch = min(SPAN_QUANT_TAPS, n_load - batch)
+                    span_grouped = sstage.tile([P, SPAN_QUANT_TAPS, G, 2], F32, align_bytes=64)
+                    for pair in range(0, n_batch, 2):
+                        n_pair = min(2, n_batch - pair)
+                        span_flip = flip.tile([P, 2, 2, G], F32, tag="flip")
+                        for k in range(n_pair):
+                            span_words = span_raw[:, batch + pair + k, :].bitcast(F32)
+                            for u in range(2):
+                                nc.tensor.transpose(span_flip[:, k, u, :], span_words[:, u * P : (u + 1) * P], ident[:])
+                        nc.scalar.copy(
+                            out=span_grouped[:, pair : pair + n_pair, :, :],
+                            in_=span_flip[:, 0:n_pair, :, :].rearrange("p k u g -> p k g u"),
+                        )
+                    taps = slice(first_tap + batch, first_tap + batch + n_batch)
                     nc.vector.quantize_mx(
-                        out=span_codes[:, tap, :].bitcast(FP8X4),
-                        scales=span_scales[:, tap, :],
-                        in_=span_grouped[:].rearrange("p g u -> p (g u)").bitcast(BF16),
+                        out=span_codes[:, taps, :].rearrange("p k g -> p (k g)").bitcast(FP8X4),
+                        scales=span_scales[:, taps, :].rearrange("p k g -> p (k g)"),
+                        in_=span_grouped[:, 0:n_batch, :, :].rearrange("p k g u -> p (k g u)").bitcast(BF16),
                     )
 
             x_codes = codes.tile([P, PASSES * PIX], U32, align_bytes=64)
@@ -125,6 +134,12 @@ def tile_involution_k_kernel(tc, x, w_reduce, b_reduce, w_span, b_span, out):
                     scales=x_scales[:, cols],
                     in_=x_grouped[:].rearrange("p q s t -> p (q s t)"),
                 )
+
+            for first_c in range(0, CH, X_PIECE):
+                chans = slice(first_c, first_c + X_PIECE)
+                x_group = xgload.tile([P, X_PIECE, PIX], BF16)
+                nc.sync.dma_start(out=x_group[:], in_=x_by_group[:, chans, :])
+                nc.vector.tensor_copy(out=x_t[:, :, chans], in_=x_group[:].rearrange("p c s -> p s c"))
 
             red_sums = [sums.tile([P, PIX], F32, name="red_sums%d" % blk, tag="sums") for blk in range(R_BLOCKS)]
             for chunk in range(CHUNKS):
@@ -198,17 +213,6 @@ def tile_involution_k_kernel(tc, x, w_reduce, b_reduce, w_span, b_span, out):
                     op=ALU.add,
                 )
 
-            for first_g in range(0, G, X_LOAD_GROUPS):
-                groups = slice(first_g, first_g + X_LOAD_GROUPS)
-                nc.sync.dma_start(out=x_chan[:, groups, :], in_=x_by_channel[:, groups, :])
-            for row in range(H):
-                if MID_FIRST_ROW + PAD <= row < MID_FIRST_ROW + MID_ROWS - PAD:
-                    continue
-                x_row_flip = flip.tile([P, W, CH], BF16, tag="flip")
-                for w in range(W):
-                    nc.tensor.transpose(x_row_flip[:, w, :], x_chan[:, :, row * W + w], ident_bf[:])
-                nc.scalar.copy(out=x_t[:, row * W : (row + 1) * W, :], in_=x_row_flip[:])
-
         block_pix = ROWS_PER_BLOCK * W
         parts = [(block * block_pix, block_pix) for block in EDGE_BLOCKS] + [(MID_FIRST_ROW * W, MID_PIX)]
         for first_pix, n_pix in parts:
@@ -255,9 +259,11 @@ def tile_involution_k_kernel(tc, x, w_reduce, b_reduce, w_span, b_span, out):
                 )
             for first_g in range(0, G, GROUPS_PER_ROUND):
                 groups = slice(first_g, first_g + GROUPS_PER_ROUND)
+                x_chan = mid.tile([P, GROUPS_PER_ROUND, PIX], BF16)
+                nc.sync.dma_start(out=x_chan[:], in_=x_by_channel[:, groups, :])
                 x_flip = xflip.tile([P, GROUPS_PER_ROUND, CH], BF16)
                 for k in range(GROUPS_PER_ROUND):
-                    nc.tensor.transpose(x_flip[:, k, :], x_chan[:, first_g + k, :], ident_bf[:])
+                    nc.tensor.transpose(x_flip[:, k, :], x_chan[:, k, :], ident_bf[:])
                 x_source = mid.tile([P, GROUPS_PER_ROUND, CH], F32)
                 nc.scalar.copy(out=x_source[:], in_=x_flip[:])
                 mid_sums = osum.tile([P, GROUPS_PER_ROUND, MID_PIX], F32)

@@ -23,7 +23,8 @@ CHUNKS = PASSES // CHUNK_PASSES
 X_CHUNK_PASSES = 4
 R_BLOCKS = R // P
 SPAN_LOAD_TAPS = 8
-SPAN_QUANT_TAPS = 4
+SPAN_BATCH = 4
+W_BUFS, X_BUFS, SPAN_BUFS = 4, 4, 2
 ROWS_PER_BLOCK = 4
 X_PIECE = 32
 RES_CHANNELS = 32
@@ -68,6 +69,7 @@ def tile_involution_k_kernel(tc, x, w_reduce, b_reduce, w_span, b_span, out):
             for first in (MID_FIRST_ROW + dh, MID_FIRST_ROW - dh):
                 nc.vector.tensor_add(out=in_window[:], in0=in_window[:], in1=same_row[:, first : first + MID_ROWS, :])
         in_window_cols = in_window[:].rearrange("p h w -> p (h w)")
+        x_group = keep.tile([P, CH, PIX], BF16)
         x_t = keep.tile([P, PIX, CH], BF16)
         prob = keep.tile([P, TAPS, PIX], F32)
         top = keep.tile([P, PIX], F32)
@@ -84,103 +86,127 @@ def tile_involution_k_kernel(tc, x, w_reduce, b_reduce, w_span, b_span, out):
         b_tap = const.tile([P, TAPS], F32)
         nc.vector.tensor_copy(out=b_tap[:], in_=b_tap_bf[:])
 
-        with tc.tile_pool(name="codes", bufs=1) as codes, tc.tile_pool(name="xstage", bufs=2) as xstage, tc.tile_pool(
-            name="wload", bufs=4
-        ) as wload, tc.tile_pool(name="wstage", bufs=2) as wstage, tc.tile_pool(name="sload", bufs=2) as sload, tc.tile_pool(
+        def gather_channels(block):
+            first_row = max(0, block * ROWS_PER_BLOCK - PAD)
+            end_row = min(H, (block + 1) * ROWS_PER_BLOCK + PAD)
+            pixels = slice(first_row * W, end_row * W)
+            for first_c in range(0, CH, X_PIECE):
+                chans = slice(first_c, first_c + X_PIECE)
+                nc.scalar.copy(out=x_t[:, pixels, chans], in_=x_group[:, chans, pixels].rearrange("p c s -> p s c"))
+
+        with tc.tile_pool(name="codes", bufs=1) as codes, tc.tile_pool(name="sload", bufs=SPAN_BUFS) as sload, tc.tile_pool(
             name="sstage", bufs=2
-        ) as sstage, tc.tile_pool(name="xgload", bufs=2) as xgload, tc.psum_pool(name="flip", bufs=4) as flip, tc.psum_pool(
-            name="sums", bufs=4
-        ) as sums:
-            span_codes = codes.tile([P, TAPS, G], U32, align_bytes=64)
-            span_scales = codes.tile([P, TAPS, G], U8, align_bytes=64)
-            for first_tap in range(0, TAPS, SPAN_LOAD_TAPS):
-                n_load = min(SPAN_LOAD_TAPS, TAPS - first_tap)
-                span_raw = sload.tile([P, SPAN_LOAD_TAPS, R], BF16)
-                nc.sync.dma_start(out=span_raw[:, 0:n_load, :], in_=span_by_group[:, first_tap : first_tap + n_load, :])
-                for batch in range(0, n_load, SPAN_QUANT_TAPS):
-                    n_batch = min(SPAN_QUANT_TAPS, n_load - batch)
-                    span_grouped = sstage.tile([P, SPAN_QUANT_TAPS, G, 2], F32, align_bytes=64)
-                    for pair in range(0, n_batch, 2):
-                        n_pair = min(2, n_batch - pair)
-                        span_flip = flip.tile([P, 2, 2, G], F32, tag="flip")
-                        for k in range(n_pair):
-                            span_words = span_raw[:, batch + pair + k, :].bitcast(F32)
-                            for u in range(2):
-                                nc.tensor.transpose(span_flip[:, k, u, :], span_words[:, u * P : (u + 1) * P], ident[:])
-                        nc.scalar.copy(
-                            out=span_grouped[:, pair : pair + n_pair, :, :],
-                            in_=span_flip[:, 0:n_pair, :, :].rearrange("p k u g -> p k g u"),
-                        )
-                    taps = slice(first_tap + batch, first_tap + batch + n_batch)
-                    nc.vector.quantize_mx(
-                        out=span_codes[:, taps, :].rearrange("p k g -> p (k g)").bitcast(FP8X4),
-                        scales=span_scales[:, taps, :].rearrange("p k g -> p (k g)"),
-                        in_=span_grouped[:, 0:n_batch, :, :].rearrange("p k g u -> p (k g u)").bitcast(BF16),
-                    )
+        ) as sstage, tc.tile_pool(name="scodes", bufs=3) as scodes, tc.tile_pool(name="xload", bufs=X_BUFS) as xload, tc.tile_pool(
+            name="xstage", bufs=2
+        ) as xstage, tc.tile_pool(name="wload", bufs=W_BUFS) as wload, tc.tile_pool(name="wstage", bufs=2) as wstage, tc.psum_pool(
+            name="flip", bufs=4
+        ) as flip, tc.psum_pool(name="sums", bufs=4) as sums, tc.manual_schedule():
 
             x_codes = codes.tile([P, PASSES * PIX], U32, align_bytes=64)
             x_scales = codes.tile([P, PASSES * PIX], U8, align_bytes=64)
-            for chunk in range(PASSES // X_CHUNK_PASSES):
-                x_raw = xstage.tile([P, X_CHUNK_PASSES, 4, PIX], BF16)
+            n_x_chunks = PASSES // X_CHUNK_PASSES
+            x_raw = {}
+            x_grouped = {}
+
+            def load_x(chunk):
+                x_raw[chunk] = xload.tile([P, X_CHUNK_PASSES, 4, PIX], BF16, name="x_raw")
                 nc.sync.dma_start(
-                    out=x_raw[:].rearrange("p q (u e) s -> p q u (e s)", u=2),
+                    out=x_raw[chunk][:].rearrange("p q (u e) s -> p q u (e s)", u=2),
                     in_=x_by_pass[:, chunk * X_CHUNK_PASSES : (chunk + 1) * X_CHUNK_PASSES],
                 )
-                x_grouped = xstage.tile([P, X_CHUNK_PASSES, PIX, 4], BF16, align_bytes=64)
-                nc.vector.tensor_copy(out=x_grouped[:], in_=x_raw[:].rearrange("p q t s -> p q s t"))
+
+            def regroup_x(chunk):
+                x_grouped[chunk] = xstage.tile([P, X_CHUNK_PASSES, PIX, 4], BF16, name="x_grouped", align_bytes=64)
+                nc.vector.tensor_copy(out=x_grouped[chunk][:], in_=x_raw[chunk][:].rearrange("p q t s -> p q s t"))
+                if chunk + X_BUFS < n_x_chunks:
+                    load_x(chunk + X_BUFS)
+
+            def quantise_x(chunk):
                 cols = slice(chunk * X_CHUNK_PASSES * PIX, (chunk + 1) * X_CHUNK_PASSES * PIX)
                 nc.vector.quantize_mx(
                     out=x_codes[:, cols].bitcast(FP8X4),
                     scales=x_scales[:, cols],
-                    in_=x_grouped[:].rearrange("p q s t -> p (q s t)"),
+                    in_=x_grouped[chunk][:].rearrange("p q s t -> p (q s t)"),
                 )
 
-            for first_c in range(0, CH, X_PIECE):
-                chans = slice(first_c, first_c + X_PIECE)
-                x_group = xgload.tile([P, X_PIECE, PIX], BF16)
-                nc.sync.dma_start(out=x_group[:], in_=x_by_group[:, chans, :])
-                nc.vector.tensor_copy(out=x_t[:, :, chans], in_=x_group[:].rearrange("p c s -> p s c"))
-
+            n_steps = CHUNKS * R_BLOCKS
             red_sums = [sums.tile([P, PIX], F32, name="red_sums%d" % blk, tag="sums") for blk in range(R_BLOCKS)]
-            for chunk in range(CHUNKS):
-                for blk in range(R_BLOCKS):
-                    w_raw = wload.tile([P, CHUNK_PASSES * K_PASS], BF16)
-                    nc.sync.dma_start(
-                        out=w_raw[:],
-                        in_=w_blocks[
-                            blk // 2, blk % 2, :, chunk * CHUNK_PASSES * K_PASS : (chunk + 1) * CHUNK_PASSES * K_PASS
-                        ],
+            w_raw = {}
+            w_grouped = {}
+            w_codes = {}
+            w_scales = {}
+
+            def load_w(step):
+                chunk, blk = step // R_BLOCKS, step % R_BLOCKS
+                w_raw[step] = wload.tile([P, CHUNK_PASSES * K_PASS], BF16, name="w_raw")
+                nc.sync.dma_start(
+                    out=w_raw[step][:],
+                    in_=w_blocks[blk // 2, blk % 2, :, chunk * CHUNK_PASSES * K_PASS : (chunk + 1) * CHUNK_PASSES * K_PASS],
+                )
+
+            def flip_w(step):
+                w_words = w_raw[step][:].bitcast(F32)
+                w_grouped[step] = wstage.tile([P, CHUNK_PASSES, P, 2], F32, name="w_grouped", align_bytes=64)
+                for pair in range(CHUNK_PASSES // 2):
+                    w_flip = flip.tile([P, 2, 2, P], F32, tag="flip")
+                    for q in range(2):
+                        for u in range(2):
+                            first = (2 * pair + q) * 2 * P + u * P
+                            nc.tensor.transpose(w_flip[:, q, u, :], w_words[:, first : first + P], ident[:])
+                    copy_out = nc.vector.tensor_copy if pair == 0 else nc.scalar.copy
+                    copy_out(
+                        out=w_grouped[step][:, 2 * pair : 2 * pair + 2, :, :], in_=w_flip[:].rearrange("p q u r -> p q r u")
                     )
-                    w_words = w_raw[:].bitcast(F32)
-                    w_grouped = wstage.tile([P, CHUNK_PASSES, P, 2], F32, align_bytes=64)
-                    for pair in range(CHUNK_PASSES // 2):
-                        w_flip = flip.tile([P, 2, 2, P], F32, tag="flip")
-                        for q in range(2):
-                            for u in range(2):
-                                first = (2 * pair + q) * 2 * P + u * P
-                                nc.tensor.transpose(w_flip[:, q, u, :], w_words[:, first : first + P], ident[:])
-                        copy_out = nc.vector.tensor_copy if pair == 0 else nc.scalar.copy
-                        copy_out(
-                            out=w_grouped[:, 2 * pair : 2 * pair + 2, :, :], in_=w_flip[:].rearrange("p q u r -> p q r u")
-                        )
-                    w_codes = wstage.tile([P, CHUNK_PASSES * P], U32, align_bytes=64)
-                    w_scales = wstage.tile([P, CHUNK_PASSES * P], U8, align_bytes=64)
-                    nc.vector.quantize_mx(
-                        out=w_codes[:].bitcast(FP8X4),
-                        scales=w_scales[:],
-                        in_=w_grouped[:].rearrange("p q r u -> p (q r u)").bitcast(BF16),
+                if step + W_BUFS < n_steps:
+                    load_w(step + W_BUFS)
+
+            def quantise_w(step):
+                w_codes[step] = wstage.tile([P, CHUNK_PASSES * P], U32, name="w_codes", align_bytes=64)
+                w_scales[step] = wstage.tile([P, CHUNK_PASSES * P], U8, name="w_scales", align_bytes=64)
+                nc.vector.quantize_mx(
+                    out=w_codes[step][:].bitcast(FP8X4),
+                    scales=w_scales[step][:],
+                    in_=w_grouped[step][:].rearrange("p q r u -> p (q r u)").bitcast(BF16),
+                )
+
+            def multiply_w(step):
+                chunk, blk = step // R_BLOCKS, step % R_BLOCKS
+                for q in range(CHUNK_PASSES):
+                    k_pass = chunk * CHUNK_PASSES + q
+                    nc.tensor.matmul_mx(
+                        out=red_sums[blk][:],
+                        lhsT=w_codes[step][:, q * P : (q + 1) * P].bitcast(FP8X4),
+                        lhsT_scale=w_scales[step][:, q * P : (q + 1) * P],
+                        rhs=x_codes[:, k_pass * PIX : (k_pass + 1) * PIX].bitcast(FP8X4),
+                        rhs_scale=x_scales[:, k_pass * PIX : (k_pass + 1) * PIX],
+                        start=(k_pass == 0),
+                        stop=(k_pass == PASSES - 1),
                     )
-                    for q in range(CHUNK_PASSES):
-                        k_pass = chunk * CHUNK_PASSES + q
-                        nc.tensor.matmul_mx(
-                            out=red_sums[blk][:],
-                            lhsT=w_codes[:, q * P : (q + 1) * P].bitcast(FP8X4),
-                            lhsT_scale=w_scales[:, q * P : (q + 1) * P],
-                            rhs=x_codes[:, k_pass * PIX : (k_pass + 1) * PIX].bitcast(FP8X4),
-                            rhs_scale=x_scales[:, k_pass * PIX : (k_pass + 1) * PIX],
-                            start=(k_pass == 0),
-                            stop=(k_pass == PASSES - 1),
-                        )
+
+            x_ahead = CHUNK_PASSES // X_CHUNK_PASSES
+            for chunk in range(x_ahead):
+                load_x(chunk)
+            for step in range(W_BUFS):
+                load_w(step)
+            for chunk in range(x_ahead, X_BUFS):
+                load_x(chunk)
+            for chunk in range(x_ahead):
+                regroup_x(chunk)
+            for chunk in range(x_ahead):
+                quantise_x(chunk)
+            for n in range(n_steps + 2):
+                x_chunk = n // 2 + x_ahead
+                with_x = n % 2 == 0 and x_chunk < n_x_chunks
+                if n < n_steps:
+                    flip_w(n)
+                if with_x:
+                    regroup_x(x_chunk)
+                if 1 <= n <= n_steps:
+                    quantise_w(n - 1)
+                if with_x:
+                    quantise_x(x_chunk)
+                if n >= 2:
+                    multiply_w(n - 2)
 
             red_grouped = codes.tile([P, PIX, R_BLOCKS], BF16, align_bytes=64)
             for blk in range(R_BLOCKS):
@@ -193,25 +219,89 @@ def tile_involution_k_kernel(tc, x, w_reduce, b_reduce, w_span, b_span, out):
                 out=red_codes[:].bitcast(FP8X4), scales=red_scales[:], in_=red_grouped[:].rearrange("p s t -> p (s t)")
             )
 
-            for first_tap in range(0, TAPS, 4):
-                n_taps = min(4, TAPS - first_tap)
-                kern_sums = sums.tile([P, 4, PIX], F32, tag="sums")
-                for k in range(n_taps):
+            n_span_loads = (TAPS + SPAN_LOAD_TAPS - 1) // SPAN_LOAD_TAPS
+            n_batches = (TAPS + SPAN_BATCH - 1) // SPAN_BATCH
+            span_raw = {}
+            span_grouped = {}
+            span_codes = {}
+            span_scales = {}
+            kern_sums = {}
+
+            def taps_of(batch):
+                return min(SPAN_BATCH, TAPS - batch * SPAN_BATCH)
+
+            def load_span(load):
+                first_tap = load * SPAN_LOAD_TAPS
+                n_load = min(SPAN_LOAD_TAPS, TAPS - first_tap)
+                span_raw[load] = sload.tile([P, SPAN_LOAD_TAPS, R], BF16, name="span_raw")
+                nc.sync.dma_start(out=span_raw[load][:, 0:n_load, :], in_=span_by_group[:, first_tap : first_tap + n_load, :])
+
+            def flip_span(batch):
+                span_grouped[batch] = sstage.tile([P, SPAN_BATCH, G, 2], F32, name="span_grouped", align_bytes=64)
+                for pair in range(0, taps_of(batch), 2):
+                    n_pair = min(2, taps_of(batch) - pair)
+                    span_flip = flip.tile([P, 2, 2, G], F32, tag="flip")
+                    for k in range(n_pair):
+                        tap = batch * SPAN_BATCH + pair + k
+                        span_words = span_raw[tap // SPAN_LOAD_TAPS][:, tap % SPAN_LOAD_TAPS, :].bitcast(F32)
+                        for u in range(2):
+                            nc.tensor.transpose(span_flip[:, k, u, :], span_words[:, u * P : (u + 1) * P], ident[:])
+                    nc.scalar.copy(
+                        out=span_grouped[batch][:, pair : pair + n_pair, :, :],
+                        in_=span_flip[:, 0:n_pair, :, :].rearrange("p k u g -> p k g u"),
+                    )
+                end_tap = batch * SPAN_BATCH + taps_of(batch)
+                if end_tap % SPAN_LOAD_TAPS == 0 and end_tap // SPAN_LOAD_TAPS - 1 + SPAN_BUFS < n_span_loads:
+                    load_span(end_tap // SPAN_LOAD_TAPS - 1 + SPAN_BUFS)
+
+            def quantise_span(batch):
+                n_taps = taps_of(batch)
+                span_codes[batch] = scodes.tile([P, SPAN_BATCH * G], U32, name="span_codes", align_bytes=64)
+                span_scales[batch] = scodes.tile([P, SPAN_BATCH * G], U8, name="span_scales", align_bytes=64)
+                nc.vector.quantize_mx(
+                    out=span_codes[batch][:, 0 : n_taps * G].bitcast(FP8X4),
+                    scales=span_scales[batch][:, 0 : n_taps * G],
+                    in_=span_grouped[batch][:, 0:n_taps, :, :].rearrange("p k g u -> p (k g u)").bitcast(BF16),
+                )
+
+            def multiply_span(batch):
+                kern_sums[batch] = sums.tile([P, SPAN_BATCH, PIX], F32, name="kern_sums", tag="sums")
+                for k in range(taps_of(batch)):
                     nc.tensor.matmul_mx(
-                        out=kern_sums[:, k, :],
-                        lhsT=span_codes[:, first_tap + k, :].bitcast(FP8X4),
-                        lhsT_scale=span_scales[:, first_tap + k, :],
+                        out=kern_sums[batch][:, k, :],
+                        lhsT=span_codes[batch][:, k * G : (k + 1) * G].bitcast(FP8X4),
+                        lhsT_scale=span_scales[batch][:, k * G : (k + 1) * G],
                         rhs=red_codes[:].bitcast(FP8X4),
                         rhs_scale=red_scales[:],
                         start=True,
                         stop=True,
                     )
+
+            def add_bias(batch):
+                n_taps = taps_of(batch)
+                taps = slice(batch * SPAN_BATCH, batch * SPAN_BATCH + n_taps)
                 nc.vector.tensor_tensor(
-                    out=prob[:, first_tap : first_tap + n_taps, :],
-                    in0=kern_sums[:, 0:n_taps, :],
-                    in1=b_tap[:, first_tap : first_tap + n_taps].unsqueeze(2).to_broadcast([P, n_taps, PIX]),
+                    out=prob[:, taps, :],
+                    in0=kern_sums[batch][:, 0:n_taps, :],
+                    in1=b_tap[:, taps].unsqueeze(2).to_broadcast([P, n_taps, PIX]),
                     op=ALU.add,
                 )
+
+            for load in range(SPAN_BUFS):
+                load_span(load)
+            for n in range(n_batches + 3):
+                if n < n_batches:
+                    flip_span(n)
+                if 1 <= n <= n_batches:
+                    quantise_span(n - 1)
+                if 2 <= n <= n_batches + 1:
+                    multiply_span(n - 2)
+                if n >= 3:
+                    add_bias(n - 3)
+
+            for first_c in range(0, CH, X_PIECE):
+                chans = slice(first_c, first_c + X_PIECE)
+                nc.sync.dma_start(out=x_group[:, chans, :], in_=x_by_group[:, chans, :])
 
         block_pix = ROWS_PER_BLOCK * W
         parts = [(block * block_pix, block_pix) for block in EDGE_BLOCKS] + [(MID_FIRST_ROW * W, MID_PIX)]
@@ -230,11 +320,26 @@ def tile_involution_k_kernel(tc, x, w_reduce, b_reduce, w_span, b_span, out):
                 out=logits, in0=logits, in1=total[:, part].unsqueeze(1).to_broadcast([P, TAPS, n_pix]), op=ALU.mult
             )
 
+        gather_channels(EDGE_BLOCKS[0])
+
         with tc.tile_pool(name="band", bufs=1) as bands, tc.tile_pool(name="mid", bufs=2) as mid, tc.psum_pool(
             name="pflip", bufs=2
         ) as pflip, tc.psum_pool(name="xflip", bufs=2) as xflip, tc.psum_pool(name="osum", bufs=2) as osum, tc.tile_pool(
             name="acc", bufs=2
         ) as accs, tc.tile_pool(name="res", bufs=3) as ress:
+            centre = PAD * KS + PAD
+
+            def start_sums(block):
+                acc = accs.tile([P, block_pix, CH], F32, name="acc")
+                for k in range(block_pix):
+                    pix = block * block_pix + k
+                    nc.scalar.activation(
+                        out=acc[:, k, :], in_=x_t[:, pix, :], func=ACT.Copy, scale=prob[:, centre, pix : pix + 1]
+                    )
+                return acc
+
+            acc_of = {EDGE_BLOCKS[0]: start_sums(EDGE_BLOCKS[0])}
+
             by_pixel = bands.tile([P, KS, SLOT_PITCH, G], F32, tag="wide")
             nc.vector.memset(by_pixel[:, :, KS, :], 0.0)
             for i in range(KS):
@@ -248,6 +353,8 @@ def tile_involution_k_kernel(tc, x, w_reduce, b_reduce, w_span, b_span, out):
                 out=out_rows[0 : PIX * SLOTS, :].rearrange("(s k) g -> s (k g)", k=SLOTS),
                 in_=by_pixel[:].rearrange("p i j g -> p (i j g)"),
             )
+            gather_channels(EDGE_BLOCKS[1])
+            acc_of[EDGE_BLOCKS[1]] = start_sums(EDGE_BLOCKS[1])
             by_source = bands.tile([P, MID_PIX, G], F32)
             for k in range(MID_PIX):
                 first = (SLOTS - 1) * (MID_FIRST_ROW * W + k) + CENTRE_SLOT
@@ -277,14 +384,9 @@ def tile_involution_k_kernel(tc, x, w_reduce, b_reduce, w_span, b_span, out):
                     out=out_by_channel[:, groups, MID_FIRST_ROW * W : MID_FIRST_ROW * W + MID_PIX], in_=mid_res[:]
                 )
 
-            centre = PAD * KS + PAD
             for block in EDGE_BLOCKS:
                 rows = range(block * ROWS_PER_BLOCK, (block + 1) * ROWS_PER_BLOCK)
-                acc = accs.tile([P, block_pix, CH], F32)
-                for pix in range(block * block_pix, (block + 1) * block_pix):
-                    nc.vector.tensor_scalar_mul(
-                        out=acc[:, pix - block * block_pix, :], in0=x_t[:, pix, :], scalar1=prob[:, centre, pix : pix + 1]
-                    )
+                acc = acc_of[block]
                 for tap in range(TAPS):
                     if tap == centre:
                         continue

@@ -27,13 +27,13 @@ SPAN_BATCH = 4
 W_BUFS, X_BUFS, SPAN_BUFS = 4, 4, 2
 ROWS_PER_BLOCK = 4
 X_PIECE = 32
-RES_CHANNELS = 32
+RES_GROUPS = 32
 EDGE_BLOCKS = (0, 3)
 MID_FIRST_ROW, MID_ROWS = 4, 8
 MID_PIX = MID_ROWS * W
-SLOT_PITCH = W
-SLOTS = KS * SLOT_PITCH
-CENTRE_SLOT = PAD * SLOT_PITCH + PAD
+QUAD = 4
+UNIT_TERMS = 16
+SCALAR_SHARE, FUSED_SHARE = 0.36, 0.38
 GROUPS_PER_ROUND = 8
 
 FLOPS = 2 * R * C * PIX + 2 * TAPS * G * R * PIX + 2 * C * PIX * TAPS
@@ -44,10 +44,8 @@ def tile_involution_k_kernel(tc, x, w_reduce, b_reduce, w_span, b_span, out):
     x_rows = x.rearrange("b c h w -> (b c) (h w)")
     x_by_pass = x_rows.rearrange("(q u p e) s -> p q u (e s)", q=PASSES, u=2, p=P, e=2)
     x_by_group = x_rows.rearrange("(g c) s -> g c s", c=CH)
-    out_by_group = out.rearrange("b (g c) h w -> g c (b h w)", c=CH)
     x_by_channel = x_rows.rearrange("(g c) s -> c g s", c=CH)
     out_by_channel = out.rearrange("b (g c) h w -> c g (b h w)", c=CH)
-    out_rows = out.rearrange("b c h w -> (b c) (h w)")
     w_blocks = w_reduce.rearrange("(u p e) c -> u e p c", u=2, p=P, e=2)
     span_by_group = w_span.rearrange("(g t) r -> g t r", t=TAPS)
 
@@ -57,18 +55,6 @@ def tile_involution_k_kernel(tc, x, w_reduce, b_reduce, w_span, b_span, out):
         ident_bf = const.tile([P, P], BF16)
         make_identity(nc, ident_bf[:])
 
-        ident_hw = ident[:].rearrange("p (h w) -> p h w", w=W)
-        same_row = const.tile([P, H, W], F32)
-        nc.vector.tensor_copy(out=same_row[:], in_=ident_hw)
-        for dw in range(1, PAD + 1):
-            nc.vector.tensor_add(out=same_row[:, :, 0 : W - dw], in0=same_row[:, :, 0 : W - dw], in1=ident_hw[:, :, dw:W])
-            nc.vector.tensor_add(out=same_row[:, :, dw:W], in0=same_row[:, :, dw:W], in1=ident_hw[:, :, 0 : W - dw])
-        in_window = const.tile([P, MID_ROWS, W], F32)
-        nc.vector.tensor_copy(out=in_window[:], in_=same_row[:, MID_FIRST_ROW : MID_FIRST_ROW + MID_ROWS, :])
-        for dh in range(1, PAD + 1):
-            for first in (MID_FIRST_ROW + dh, MID_FIRST_ROW - dh):
-                nc.vector.tensor_add(out=in_window[:], in0=in_window[:], in1=same_row[:, first : first + MID_ROWS, :])
-        in_window_cols = in_window[:].rearrange("p h w -> p (h w)")
         x_group = keep.tile([P, CH, PIX], BF16)
         x_t = keep.tile([P, PIX, CH], BF16)
         prob = keep.tile([P, TAPS, PIX], F32)
@@ -304,109 +290,207 @@ def tile_involution_k_kernel(tc, x, w_reduce, b_reduce, w_span, b_span, out):
                 nc.sync.dma_start(out=x_group[:, chans, :], in_=x_by_group[:, chans, :])
 
         block_pix = ROWS_PER_BLOCK * W
-        parts = [(block * block_pix, block_pix) for block in EDGE_BLOCKS] + [(MID_FIRST_ROW * W, MID_PIX)]
-        for first_pix, n_pix in parts:
+        mid_first = MID_FIRST_ROW * W
+        prob_ij = prob[:].rearrange("p (i j) s -> p i j s", j=KS)
+
+        def softmax_in(first_pix, n_pix):
             part = slice(first_pix, first_pix + n_pix)
             logits = prob[:, :, part]
-            by_tap_last = logits.rearrange("p t s -> p s t")
-            nc.vector.tensor_reduce(out=top[:, part], in_=by_tap_last, axis=AXIS.X, op=ALU.max)
+            nc.vector.tensor_reduce(out=top[:, part], in_=logits.rearrange("p t s -> p s t"), axis=AXIS.X, op=ALU.max)
             nc.vector.tensor_tensor(
                 out=logits, in0=logits, in1=top[:, part].unsqueeze(1).to_broadcast([P, TAPS, n_pix]), op=ALU.subtract
             )
+
+        def softmax_exp(first_pix, n_pix):
+            logits = prob[:, :, first_pix : first_pix + n_pix]
             nc.scalar.activation(out=logits, in_=logits, func=ACT.Exp)
-            nc.vector.tensor_reduce(out=total[:, part], in_=by_tap_last, axis=AXIS.X, op=ALU.add)
+
+        def softmax_total(first_pix, n_pix):
+            part = slice(first_pix, first_pix + n_pix)
+            nc.vector.tensor_reduce(
+                out=total[:, part], in_=prob[:, :, part].rearrange("p t s -> p s t"), axis=AXIS.X, op=ALU.add
+            )
             nc.vector.reciprocal(out=total[:, part], in_=total[:, part])
+
+        def softmax_out(first_pix, n_pix):
+            part = slice(first_pix, first_pix + n_pix)
+            logits = prob[:, :, part]
             nc.vector.tensor_tensor(
                 out=logits, in0=logits, in1=total[:, part].unsqueeze(1).to_broadcast([P, TAPS, n_pix]), op=ALU.mult
             )
 
-        gather_channels(EDGE_BLOCKS[0])
-
         with tc.tile_pool(name="band", bufs=1) as bands, tc.tile_pool(name="mid", bufs=2) as mid, tc.psum_pool(
-            name="pflip", bufs=2
-        ) as pflip, tc.psum_pool(name="xflip", bufs=2) as xflip, tc.psum_pool(name="osum", bufs=2) as osum, tc.tile_pool(
-            name="acc", bufs=2
-        ) as accs, tc.tile_pool(name="res", bufs=3) as ress:
-            centre = PAD * KS + PAD
-
-            def start_sums(block):
-                acc = accs.tile([P, block_pix, CH], F32, name="acc")
-                for k in range(block_pix):
-                    pix = block * block_pix + k
-                    nc.scalar.activation(
-                        out=acc[:, k, :], in_=x_t[:, pix, :], func=ACT.Copy, scale=prob[:, centre, pix : pix + 1]
-                    )
-                return acc
-
-            acc_of = {EDGE_BLOCKS[0]: start_sums(EDGE_BLOCKS[0])}
-
-            by_pixel = bands.tile([P, KS, SLOT_PITCH, G], F32, tag="wide")
-            nc.vector.memset(by_pixel[:, :, KS, :], 0.0)
-            for i in range(KS):
-                for first_j in range(0, KS, 4):
-                    n_taps = min(4, KS - first_j)
-                    prob_flip = pflip.tile([P, 4, G], F32)
-                    for k in range(n_taps):
-                        nc.tensor.transpose(prob_flip[:, k, :], prob[:, i * KS + first_j + k, :], ident[:])
-                    nc.scalar.copy(out=by_pixel[:, i, first_j : first_j + n_taps, :], in_=prob_flip[:, 0:n_taps, :])
-            nc.sync.dma_start(
-                out=out_rows[0 : PIX * SLOTS, :].rearrange("(s k) g -> s (k g)", k=SLOTS),
-                in_=by_pixel[:].rearrange("p i j g -> p (i j g)"),
-            )
-            gather_channels(EDGE_BLOCKS[1])
-            acc_of[EDGE_BLOCKS[1]] = start_sums(EDGE_BLOCKS[1])
-            by_source = bands.tile([P, MID_PIX, G], F32)
-            for k in range(MID_PIX):
-                first = (SLOTS - 1) * (MID_FIRST_ROW * W + k) + CENTRE_SLOT
-                nc.sync.dma_start(out=by_source[:, k, :], in_=out_rows[first : first + PIX, :])
-            band = bands.tile([P, G, MID_PIX], F32, tag="wide")
-            for k in range(MID_PIX):
-                nc.scalar.activation(
-                    out=band[:, :, k], in_=by_source[:, k, :], func=ACT.Copy, scale=in_window_cols[:, k : k + 1]
+            name="flip2", bufs=2
+        ) as flip2, tc.psum_pool(name="xflip", bufs=2) as xflip, tc.psum_pool(name="osum", bufs=2) as osum, tc.psum_pool(
+            name="quads", bufs=2
+        ) as quads, tc.tile_pool(name="prods", bufs=4) as prods, tc.tile_pool(name="res", bufs=2) as ress, tc.manual_schedule():
+            edge_parts = [(block * block_pix, block_pix) for block in EDGE_BLOCKS]
+            spread = bands.tile([P, MID_PIX, PIX], F32)
+            nc.gpsimd.memset(spread[:], 0.0)
+            spread_hw = spread[:].rearrange("p m (h w) -> p m h w", w=W)
+            softmax_in(mid_first, MID_PIX)
+            gather_channels(EDGE_BLOCKS[0])
+            softmax_exp(mid_first, MID_PIX)
+            softmax_in(edge_parts[0][0], block_pix)
+            softmax_exp(edge_parts[0][0], block_pix)
+            softmax_total(mid_first, MID_PIX)
+            for m in range(MID_PIX):
+                h, w = MID_FIRST_ROW + m // W, m % W
+                first_j, end_j = max(0, PAD - w), min(KS, W + PAD - w)
+                nc.vector.tensor_scalar(
+                    out=spread_hw[:, m, h - PAD : h + PAD + 1, w + first_j - PAD : w + end_j - PAD],
+                    in0=prob_ij[:, :, first_j:end_j, mid_first + m],
+                    scalar1=total[:, mid_first + m : mid_first + m + 1],
+                    scalar2=None,
+                    op0=ALU.mult,
                 )
-            for first_g in range(0, G, GROUPS_PER_ROUND):
-                groups = slice(first_g, first_g + GROUPS_PER_ROUND)
-                x_chan = mid.tile([P, GROUPS_PER_ROUND, PIX], BF16)
-                nc.sync.dma_start(out=x_chan[:], in_=x_by_channel[:, groups, :])
+            softmax_total(edge_parts[0][0], block_pix)
+            softmax_out(edge_parts[0][0], block_pix)
+            gather_channels(EDGE_BLOCKS[1])
+            softmax_in(edge_parts[1][0], block_pix)
+            softmax_exp(edge_parts[1][0], block_pix)
+            softmax_total(edge_parts[1][0], block_pix)
+            softmax_out(edge_parts[1][0], block_pix)
+
+            band = bands.tile([P, G, MID_PIX], F32)
+            for first in range(0, MID_PIX, QUAD):
+                spread_flip = flip2.tile([P, QUAD, G], F32)
+                for k in range(QUAD):
+                    nc.tensor.transpose(spread_flip[:, k, :], spread[:, first + k, :], ident[:])
+                nc.scalar.copy(out=band[:, :, first : first + QUAD], in_=spread_flip[:].rearrange("p k g -> p g k"))
+
+            n_rounds = G // GROUPS_PER_ROUND
+            x_chan = {}
+            x_source = {}
+            mid_sums = {}
+
+            def load_chan(rnd):
+                x_chan[rnd] = mid.tile([P, GROUPS_PER_ROUND, PIX], BF16, name="x_chan")
+                groups = slice(rnd * GROUPS_PER_ROUND, (rnd + 1) * GROUPS_PER_ROUND)
+                nc.sync.dma_start(out=x_chan[rnd][:], in_=x_by_channel[:, groups, :])
+
+            def flip_chan(rnd):
                 x_flip = xflip.tile([P, GROUPS_PER_ROUND, CH], BF16)
                 for k in range(GROUPS_PER_ROUND):
-                    nc.tensor.transpose(x_flip[:, k, :], x_chan[:, k, :], ident_bf[:])
-                x_source = mid.tile([P, GROUPS_PER_ROUND, CH], F32)
-                nc.scalar.copy(out=x_source[:], in_=x_flip[:])
-                mid_sums = osum.tile([P, GROUPS_PER_ROUND, MID_PIX], F32)
+                    nc.tensor.transpose(x_flip[:, k, :], x_chan[rnd][:, k, :], ident_bf[:])
+                x_source[rnd] = mid.tile([P, GROUPS_PER_ROUND, CH], F32, name="x_source")
+                nc.scalar.copy(out=x_source[rnd][:], in_=x_flip[:])
+
+            def multiply_band(rnd):
+                mid_sums[rnd] = osum.tile([P, GROUPS_PER_ROUND, MID_PIX], F32, name="mid_sums")
                 for k in range(GROUPS_PER_ROUND):
                     nc.tensor.matmul(
-                        out=mid_sums[:, k, :], lhsT=x_source[:, k, :], rhs=band[:, first_g + k, :], start=True, stop=True
+                        out=mid_sums[rnd][:, k, :],
+                        lhsT=x_source[rnd][:, k, :],
+                        rhs=band[:, rnd * GROUPS_PER_ROUND + k, :],
+                        start=True,
+                        stop=True,
                     )
-                mid_res = mid.tile([P, GROUPS_PER_ROUND, MID_PIX], F32)
-                nc.scalar.copy(out=mid_res[:], in_=mid_sums[:])
-                nc.sync.dma_start(
-                    out=out_by_channel[:, groups, MID_FIRST_ROW * W : MID_FIRST_ROW * W + MID_PIX], in_=mid_res[:]
-                )
 
+            def store_band(rnd):
+                mid_res = mid.tile([P, GROUPS_PER_ROUND, MID_PIX], F32)
+                nc.scalar.copy(out=mid_res[:], in_=mid_sums[rnd][:])
+                groups = slice(rnd * GROUPS_PER_ROUND, (rnd + 1) * GROUPS_PER_ROUND)
+                nc.sync.dma_start(out=out_by_channel[:, groups, mid_first : mid_first + MID_PIX], in_=mid_res[:])
+
+            units = []
             for block in EDGE_BLOCKS:
-                rows = range(block * ROWS_PER_BLOCK, (block + 1) * ROWS_PER_BLOCK)
-                acc = acc_of[block]
-                for tap in range(TAPS):
-                    if tap == centre:
-                        continue
-                    dh, dw = tap // KS - PAD, tap % KS - PAD
-                    for h in rows:
-                        for w in range(W):
-                            if not (0 <= h + dh < H and 0 <= w + dw < W):
-                                continue
-                            pix = h * W + w
-                            mine = acc[:, pix - block * block_pix, :]
-                            nc.vector.scalar_tensor_tensor(
-                                out=mine,
-                                in0=x_t[:, (h + dh) * W + w + dw, :],
-                                scalar=prob[:, tap, pix : pix + 1],
-                                in1=mine,
-                                op0=ALU.mult,
-                                op1=ALU.add,
-                            )
-                for first_c in range(0, CH, RES_CHANNELS):
-                    chans = slice(first_c, first_c + RES_CHANNELS)
-                    res = ress.tile([P, RES_CHANNELS, block_pix], F32)
-                    nc.scalar.copy(out=res[:], in_=acc[:, :, chans].rearrange("p s c -> p c s"))
-                    nc.sync.dma_start(out=out_by_group[:, chans, block * block_pix : (block + 1) * block_pix], in_=res[:])
+                for pix in range(block * block_pix, (block + 1) * block_pix):
+                    h, w = pix // W, pix % W
+                    terms = []
+                    for tap in range(TAPS):
+                        source_h, source_w = h + tap // KS - PAD, w + tap % KS - PAD
+                        if 0 <= source_h < H and 0 <= source_w < W:
+                            terms.append((tap, source_h * W + source_w))
+                    n_units = (len(terms) + UNIT_TERMS - 1) // UNIT_TERMS
+                    for u in range(n_units):
+                        part = terms[u * len(terms) // n_units : (u + 1) * len(terms) // n_units]
+                        units.append((pix, part, u == 0, u == n_units - 1))
+            made = {}
+            quad_sums = {}
+            block_res = {}
+
+            def counts(u):
+                n = len(units[u][1])
+                n_scalar = round(SCALAR_SHARE * n)
+                n_fused = round(FUSED_SHARE * n)
+                return n_scalar, n - n_scalar - n_fused, n_fused
+
+            def make_products(u):
+                pix, terms = units[u][0], units[u][1]
+                n_scalar, n_vector, n_fused = counts(u)
+                made[u] = prods.tile([P, UNIT_TERMS, CH], F32, name="made")
+                for k in range(n_scalar + n_vector):
+                    tap, source = terms[k]
+                    weight = prob[:, tap, pix : pix + 1]
+                    if k < n_scalar:
+                        nc.scalar.activation(out=made[u][:, k, :], in_=x_t[:, source, :], func=ACT.Copy, scale=weight)
+                    else:
+                        nc.vector.tensor_scalar(
+                            out=made[u][:, k, :], in0=x_t[:, source, :], scalar1=weight, scalar2=None, op0=ALU.mult
+                        )
+
+            def fuse_products(u):
+                pix, terms = units[u][0], units[u][1]
+                n_scalar, n_vector, n_fused = counts(u)
+                for k in range(n_fused):
+                    tap, source = terms[n_scalar + n_vector + k]
+                    mine = made[u][:, k, :]
+                    nc.vector.scalar_tensor_tensor(
+                        out=mine, in0=x_t[:, source, :], scalar=prob[:, tap, pix : pix + 1], in1=mine, op0=ALU.mult, op1=ALU.add
+                    )
+
+            def sum_products(u):
+                pix, first, last = units[u][0], units[u][2], units[u][3]
+                n_scalar, n_vector, n_fused = counts(u)
+                n_made = n_scalar + n_vector
+                if first and pix % QUAD == 0:
+                    quad_sums[pix // QUAD] = quads.tile([P, QUAD, G], F32, name="quad_sums")
+                for k in range(n_made):
+                    nc.tensor.matmul(
+                        out=quad_sums[pix // QUAD][:, pix % QUAD, :],
+                        lhsT=made[u][:, k, :],
+                        rhs=ident[:],
+                        is_transpose=True,
+                        start=(first and k == 0),
+                        stop=(last and k == n_made - 1),
+                    )
+
+            def store_quad(quad):
+                block = quad * QUAD // block_pix
+                if quad * QUAD % block_pix == 0:
+                    block_res[block] = ress.tile([P, G, block_pix], F32, name="block_res")
+                first = quad * QUAD - block * block_pix
+                nc.scalar.copy(
+                    out=block_res[block][:, :, first : first + QUAD], in_=quad_sums[quad][:].rearrange("p k g -> p g k")
+                )
+                if first + QUAD == block_pix:
+                    for first_g in range(0, G, RES_GROUPS):
+                        groups = slice(first_g, first_g + RES_GROUPS)
+                        nc.sync.dma_start(
+                            out=out_by_channel[:, groups, block * block_pix : (block + 1) * block_pix],
+                            in_=block_res[block][:, groups, :],
+                        )
+
+            load_chan(0)
+            load_chan(1)
+            flip_chan(0)
+            rnd = 0
+            n_units = len(units)
+            for u in range(n_units + 1):
+                if u < n_units:
+                    make_products(u)
+                if 1 <= u <= n_units:
+                    fuse_products(u - 1)
+                    sum_products(u - 1)
+                    if units[u - 1][3] and units[u - 1][0] % QUAD == QUAD - 1:
+                        if rnd + 2 < n_rounds:
+                            load_chan(rnd + 2)
+                        if rnd + 1 < n_rounds:
+                            flip_chan(rnd + 1)
+                        multiply_band(rnd)
+                        store_quad(units[u - 1][0] // QUAD)
+                        if rnd >= 1:
+                            store_band(rnd - 1)
+                        rnd += 1
+            store_band(n_rounds - 1)

@@ -361,6 +361,7 @@ def tile_involution_k_kernel(tc, x, w_reduce, b_reduce, w_span, b_span, out):
 
             n_rounds = G // GROUPS_PER_ROUND
             x_chan = {}
+            x_flip = {}
             x_source = {}
             mid_sums = {}
 
@@ -369,23 +370,25 @@ def tile_involution_k_kernel(tc, x, w_reduce, b_reduce, w_span, b_span, out):
                 groups = slice(rnd * GROUPS_PER_ROUND, (rnd + 1) * GROUPS_PER_ROUND)
                 nc.sync.dma_start(out=x_chan[rnd][:], in_=x_by_channel[:, groups, :])
 
-            def flip_chan(rnd):
-                x_flip = xflip.tile([P, GROUPS_PER_ROUND, CH], BF16)
-                for k in range(GROUPS_PER_ROUND):
-                    nc.tensor.transpose(x_flip[:, k, :], x_chan[rnd][:, k, :], ident_bf[:])
-                x_source[rnd] = mid.tile([P, GROUPS_PER_ROUND, CH], F32, name="x_source")
-                nc.scalar.copy(out=x_source[rnd][:], in_=x_flip[:])
+            def flip_chan(group):
+                rnd, k = group // GROUPS_PER_ROUND, group % GROUPS_PER_ROUND
+                if k == 0:
+                    x_flip[rnd] = xflip.tile([P, GROUPS_PER_ROUND, CH], BF16, name="x_flip")
+                nc.tensor.transpose(x_flip[rnd][:, k, :], x_chan[rnd][:, k, :], ident_bf[:])
+                if k == GROUPS_PER_ROUND - 1 and rnd + 2 < n_rounds:
+                    load_chan(rnd + 2)
 
-            def multiply_band(rnd):
-                mid_sums[rnd] = osum.tile([P, GROUPS_PER_ROUND, MID_PIX], F32, name="mid_sums")
-                for k in range(GROUPS_PER_ROUND):
-                    nc.tensor.matmul(
-                        out=mid_sums[rnd][:, k, :],
-                        lhsT=x_source[rnd][:, k, :],
-                        rhs=band[:, rnd * GROUPS_PER_ROUND + k, :],
-                        start=True,
-                        stop=True,
-                    )
+            def copy_source(rnd):
+                x_source[rnd] = mid.tile([P, GROUPS_PER_ROUND, CH], F32, name="x_source")
+                nc.scalar.copy(out=x_source[rnd][:], in_=x_flip[rnd][:])
+
+            def multiply_band(group):
+                rnd, k = group // GROUPS_PER_ROUND, group % GROUPS_PER_ROUND
+                if k == 0:
+                    mid_sums[rnd] = osum.tile([P, GROUPS_PER_ROUND, MID_PIX], F32, name="mid_sums")
+                nc.tensor.matmul(
+                    out=mid_sums[rnd][:, k, :], lhsT=x_source[rnd][:, k, :], rhs=band[:, group, :], start=True, stop=True
+                )
 
             def store_band(rnd):
                 mid_res = mid.tile([P, GROUPS_PER_ROUND, MID_PIX], F32)
@@ -474,23 +477,28 @@ def tile_involution_k_kernel(tc, x, w_reduce, b_reduce, w_span, b_span, out):
 
             load_chan(0)
             load_chan(1)
-            flip_chan(0)
-            rnd = 0
+            flip_lead = GROUPS_PER_ROUND + 2
+            for group in range(flip_lead):
+                flip_chan(group)
+            copy_source(0)
+            group = 0
             n_units = len(units)
             for u in range(n_units + 1):
                 if u < n_units:
                     make_products(u)
-                if 1 <= u <= n_units:
+                if 1 <= u:
                     fuse_products(u - 1)
                     sum_products(u - 1)
-                    if units[u - 1][3] and units[u - 1][0] % QUAD == QUAD - 1:
-                        if rnd + 2 < n_rounds:
-                            load_chan(rnd + 2)
-                        if rnd + 1 < n_rounds:
-                            flip_chan(rnd + 1)
-                        multiply_band(rnd)
-                        store_quad(units[u - 1][0] // QUAD)
-                        if rnd >= 1:
-                            store_band(rnd - 1)
-                        rnd += 1
+                    while group < G and group * n_units < u * G:
+                        if group + flip_lead < G:
+                            flip_chan(group + flip_lead)
+                        if group % GROUPS_PER_ROUND == GROUPS_PER_ROUND - 1 and group + 1 < G:
+                            copy_source((group + 1) // GROUPS_PER_ROUND)
+                        multiply_band(group)
+                        if group % GROUPS_PER_ROUND == 1 and group > GROUPS_PER_ROUND:
+                            store_band(group // GROUPS_PER_ROUND - 1)
+                        group += 1
+                if u >= 2 and units[u - 2][3] and units[u - 2][0] % QUAD == QUAD - 1:
+                    store_quad(units[u - 2][0] // QUAD)
+            store_quad(units[n_units - 1][0] // QUAD)
             store_band(n_rounds - 1)

@@ -25,16 +25,17 @@ R_BLOCKS = R // P
 SPAN_LOAD_TAPS = 8
 SPAN_BATCH = 4
 W_BUFS, X_BUFS, SPAN_BUFS = 4, 4, 2
-ROWS_PER_BLOCK = 4
+BLOCK_PIX = 32
 X_PIECE = 32
 RES_GROUPS = 32
-EDGE_BLOCKS = (0, 3)
-MID_FIRST_ROW, MID_ROWS = 4, 8
-MID_PIX = MID_ROWS * W
+BAND_FIRST, BAND_PIX = 32, 70
+BAND_PITCH = 72
+BAND_STORE = 64
+TAP_PITCH = 52
 QUAD = 4
 UNIT_TERMS = 16
-SCALAR_SHARE, FUSED_SHARE = 0.36, 0.38
-GROUPS_PER_ROUND = 8
+SCALAR_SHARE, FUSED_SHARE = 0.34, 0.36
+GROUPS_PER_ROUND = 7
 
 FLOPS = 2 * R * C * PIX + 2 * TAPS * G * R * PIX + 2 * C * PIX * TAPS
 
@@ -57,7 +58,7 @@ def tile_involution_k_kernel(tc, x, w_reduce, b_reduce, w_span, b_span, out):
 
         x_group = keep.tile([P, CH, PIX], BF16)
         x_t = keep.tile([P, PIX, CH], BF16)
-        prob = keep.tile([P, TAPS, PIX], F32)
+        weights = keep.tile([P, PIX, TAP_PITCH], F32)
         top = keep.tile([P, PIX], F32)
         total = keep.tile([P, PIX], F32)
 
@@ -72,13 +73,10 @@ def tile_involution_k_kernel(tc, x, w_reduce, b_reduce, w_span, b_span, out):
         b_tap = const.tile([P, TAPS], F32)
         nc.vector.tensor_copy(out=b_tap[:], in_=b_tap_bf[:])
 
-        def gather_channels(block):
-            first_row = max(0, block * ROWS_PER_BLOCK - PAD)
-            end_row = min(H, (block + 1) * ROWS_PER_BLOCK + PAD)
+        def gather_channels(copy, first_row, end_row, piece):
             pixels = slice(first_row * W, end_row * W)
-            for first_c in range(0, CH, X_PIECE):
-                chans = slice(first_c, first_c + X_PIECE)
-                nc.scalar.copy(out=x_t[:, pixels, chans], in_=x_group[:, chans, pixels].rearrange("p c s -> p s c"))
+            chans = slice(piece * X_PIECE, (piece + 1) * X_PIECE)
+            copy(out=x_t[:, pixels, chans], in_=x_group[:, chans, pixels].rearrange("p c s -> p s c"))
 
         with tc.tile_pool(name="codes", bufs=1) as codes, tc.tile_pool(name="sload", bufs=SPAN_BUFS) as sload, tc.tile_pool(
             name="sstage", bufs=2
@@ -267,9 +265,9 @@ def tile_involution_k_kernel(tc, x, w_reduce, b_reduce, w_span, b_span, out):
                 n_taps = taps_of(batch)
                 taps = slice(batch * SPAN_BATCH, batch * SPAN_BATCH + n_taps)
                 nc.vector.tensor_tensor(
-                    out=prob[:, taps, :],
-                    in0=kern_sums[batch][:, 0:n_taps, :],
-                    in1=b_tap[:, taps].unsqueeze(2).to_broadcast([P, n_taps, PIX]),
+                    out=weights[:, :, taps],
+                    in0=kern_sums[batch][:, 0:n_taps, :].rearrange("p k s -> p s k"),
+                    in1=b_tap[:, taps].unsqueeze(1).to_broadcast([P, PIX, n_taps]),
                     op=ALU.add,
                 )
 
@@ -289,129 +287,136 @@ def tile_involution_k_kernel(tc, x, w_reduce, b_reduce, w_span, b_span, out):
                 chans = slice(first_c, first_c + X_PIECE)
                 nc.sync.dma_start(out=x_group[:, chans, :], in_=x_by_group[:, chans, :])
 
-        block_pix = ROWS_PER_BLOCK * W
-        mid_first = MID_FIRST_ROW * W
-        prob_ij = prob[:].rearrange("p (i j) s -> p i j s", j=KS)
+        end_band = BAND_FIRST + BAND_PIX
+        first_tail = PIX - BLOCK_PIX
 
-        def softmax_in(first_pix, n_pix):
-            part = slice(first_pix, first_pix + n_pix)
-            logits = prob[:, :, part]
-            nc.vector.tensor_reduce(out=top[:, part], in_=logits.rearrange("p t s -> p s t"), axis=AXIS.X, op=ALU.max)
-            nc.vector.tensor_tensor(
-                out=logits, in0=logits, in1=top[:, part].unsqueeze(1).to_broadcast([P, TAPS, n_pix]), op=ALU.subtract
+        def find_top(first_pix, end_pix):
+            part = slice(first_pix, end_pix)
+            nc.vector.tensor_reduce(out=top[:, part], in_=weights[:, part, 0:TAPS], axis=AXIS.X, op=ALU.max)
+            nc.vector.tensor_scalar(out=top[:, part], in0=top[:, part], scalar1=-1.0, scalar2=None, op0=ALU.mult)
+
+        def exponentials(pix):
+            logits = weights[:, pix, 0:TAPS]
+            nc.scalar.activation(
+                out=logits, in_=logits, func=ACT.Exp, bias=top[:, pix : pix + 1], scale=1.0, accum_out=total[:, pix : pix + 1]
             )
 
-        def softmax_exp(first_pix, n_pix):
-            logits = prob[:, :, first_pix : first_pix + n_pix]
-            nc.scalar.activation(out=logits, in_=logits, func=ACT.Exp)
-
-        def softmax_total(first_pix, n_pix):
-            part = slice(first_pix, first_pix + n_pix)
-            nc.vector.tensor_reduce(
-                out=total[:, part], in_=prob[:, :, part].rearrange("p t s -> p s t"), axis=AXIS.X, op=ALU.add
-            )
+        def normalise(first_pix, end_pix):
+            part = slice(first_pix, end_pix)
             nc.vector.reciprocal(out=total[:, part], in_=total[:, part])
-
-        def softmax_out(first_pix, n_pix):
-            part = slice(first_pix, first_pix + n_pix)
-            logits = prob[:, :, part]
             nc.vector.tensor_tensor(
-                out=logits, in0=logits, in1=total[:, part].unsqueeze(1).to_broadcast([P, TAPS, n_pix]), op=ALU.mult
+                out=weights[:, part, 0:TAPS],
+                in0=weights[:, part, 0:TAPS],
+                in1=total[:, part].unsqueeze(2).to_broadcast([P, end_pix - first_pix, TAPS]),
+                op=ALU.mult,
             )
 
         with tc.tile_pool(name="band", bufs=1) as bands, tc.tile_pool(name="mid", bufs=2) as mid, tc.psum_pool(
             name="flip2", bufs=2
         ) as flip2, tc.psum_pool(name="xflip", bufs=2) as xflip, tc.psum_pool(name="osum", bufs=2) as osum, tc.psum_pool(
             name="quads", bufs=2
-        ) as quads, tc.tile_pool(name="prods", bufs=4) as prods, tc.tile_pool(name="res", bufs=2) as ress, tc.manual_schedule():
-            edge_parts = [(block * block_pix, block_pix) for block in EDGE_BLOCKS]
-            spread = bands.tile([P, MID_PIX, PIX], F32)
+        ) as quads, tc.tile_pool(name="prods", bufs=4) as prods, tc.tile_pool(name="res", bufs=1) as ress, tc.manual_schedule():
+            spread = bands.tile([P, BAND_PIX, PIX], F32)
             nc.gpsimd.memset(spread[:], 0.0)
             spread_hw = spread[:].rearrange("p m (h w) -> p m h w", w=W)
-            softmax_in(mid_first, MID_PIX)
-            gather_channels(EDGE_BLOCKS[0])
-            softmax_exp(mid_first, MID_PIX)
-            softmax_in(edge_parts[0][0], block_pix)
-            softmax_exp(edge_parts[0][0], block_pix)
-            softmax_total(mid_first, MID_PIX)
-            for m in range(MID_PIX):
-                h, w = MID_FIRST_ROW + m // W, m % W
+            band = bands.tile([P, G, BAND_PITCH], F32)
+            spread_flip = {}
+
+            def spread_weights(m):
+                pix = BAND_FIRST + m
+                h, w = pix // W, pix % W
                 first_j, end_j = max(0, PAD - w), min(KS, W + PAD - w)
+                end_i = min(KS, H + PAD - h)
                 nc.vector.tensor_scalar(
-                    out=spread_hw[:, m, h - PAD : h + PAD + 1, w + first_j - PAD : w + end_j - PAD],
-                    in0=prob_ij[:, :, first_j:end_j, mid_first + m],
-                    scalar1=total[:, mid_first + m : mid_first + m + 1],
+                    out=spread_hw[:, m, h - PAD : h - PAD + end_i, w + first_j - PAD : w + end_j - PAD],
+                    in0=weights[:, pix, 0:TAPS].rearrange("p (i j) -> p i j", j=KS)[:, 0:end_i, first_j:end_j],
+                    scalar1=total[:, pix : pix + 1],
                     scalar2=None,
                     op0=ALU.mult,
                 )
-            softmax_total(edge_parts[0][0], block_pix)
-            softmax_out(edge_parts[0][0], block_pix)
-            gather_channels(EDGE_BLOCKS[1])
-            softmax_in(edge_parts[1][0], block_pix)
-            softmax_exp(edge_parts[1][0], block_pix)
-            softmax_total(edge_parts[1][0], block_pix)
-            softmax_out(edge_parts[1][0], block_pix)
 
-            band = bands.tile([P, G, MID_PIX], F32)
-            for first in range(0, MID_PIX, QUAD):
-                spread_flip = flip2.tile([P, QUAD, G], F32)
-                for k in range(QUAD):
-                    nc.tensor.transpose(spread_flip[:, k, :], spread[:, first + k, :], ident[:])
-                nc.scalar.copy(out=band[:, :, first : first + QUAD], in_=spread_flip[:].rearrange("p k g -> p g k"))
+            n_band_quads = (BAND_PIX + QUAD - 1) // QUAD
 
-            n_rounds = G // GROUPS_PER_ROUND
+            def flip_spread(quad):
+                spread_flip[quad] = flip2.tile([P, QUAD, G], F32, name="spread_flip")
+                for k in range(min(QUAD, BAND_PIX - quad * QUAD)):
+                    nc.tensor.transpose(spread_flip[quad][:, k, :], spread[:, quad * QUAD + k, :], ident[:])
+
+            def copy_band(quad):
+                n_pix = min(QUAD, BAND_PIX - quad * QUAD)
+                nc.scalar.copy(
+                    out=band[:, :, quad * QUAD : quad * QUAD + n_pix],
+                    in_=spread_flip[quad][:, 0:n_pix, :].rearrange("p k g -> p g k"),
+                )
+
+            n_rounds = (G + GROUPS_PER_ROUND - 1) // GROUPS_PER_ROUND
             x_chan = {}
             x_flip = {}
             x_source = {}
             mid_sums = {}
+            head_res = ress.tile([P, G, BLOCK_PIX], F32)
+            tail_res = ress.tile([P, G, BLOCK_PIX], F32)
+
+            def groups_of(rnd):
+                return slice(rnd * GROUPS_PER_ROUND, min(G, (rnd + 1) * GROUPS_PER_ROUND))
+
+            def n_groups_of(rnd):
+                return min(GROUPS_PER_ROUND, G - rnd * GROUPS_PER_ROUND)
 
             def load_chan(rnd):
                 x_chan[rnd] = mid.tile([P, GROUPS_PER_ROUND, PIX], BF16, name="x_chan")
-                groups = slice(rnd * GROUPS_PER_ROUND, (rnd + 1) * GROUPS_PER_ROUND)
-                nc.sync.dma_start(out=x_chan[rnd][:], in_=x_by_channel[:, groups, :])
+                nc.sync.dma_start(out=x_chan[rnd][:, 0 : n_groups_of(rnd), :], in_=x_by_channel[:, groups_of(rnd), :])
 
             def flip_chan(group):
                 rnd, k = group // GROUPS_PER_ROUND, group % GROUPS_PER_ROUND
                 if k == 0:
                     x_flip[rnd] = xflip.tile([P, GROUPS_PER_ROUND, CH], BF16, name="x_flip")
                 nc.tensor.transpose(x_flip[rnd][:, k, :], x_chan[rnd][:, k, :], ident_bf[:])
-                if k == GROUPS_PER_ROUND - 1 and rnd + 2 < n_rounds:
+                if k == n_groups_of(rnd) - 1 and rnd + 2 < n_rounds:
                     load_chan(rnd + 2)
 
             def copy_source(rnd):
                 x_source[rnd] = mid.tile([P, GROUPS_PER_ROUND, CH], F32, name="x_source")
-                nc.scalar.copy(out=x_source[rnd][:], in_=x_flip[rnd][:])
+                nc.scalar.copy(out=x_source[rnd][:, 0 : n_groups_of(rnd), :], in_=x_flip[rnd][:, 0 : n_groups_of(rnd), :])
 
             def multiply_band(group):
                 rnd, k = group // GROUPS_PER_ROUND, group % GROUPS_PER_ROUND
                 if k == 0:
-                    mid_sums[rnd] = osum.tile([P, GROUPS_PER_ROUND, MID_PIX], F32, name="mid_sums")
+                    mid_sums[rnd] = osum.tile([P, GROUPS_PER_ROUND, BAND_PIX], F32, name="mid_sums")
                 nc.tensor.matmul(
-                    out=mid_sums[rnd][:, k, :], lhsT=x_source[rnd][:, k, :], rhs=band[:, group, :], start=True, stop=True
+                    out=mid_sums[rnd][:, k, :],
+                    lhsT=x_source[rnd][:, k, :],
+                    rhs=band[:, group, 0:BAND_PIX],
+                    start=True,
+                    stop=True,
                 )
 
             def store_band(rnd):
-                mid_res = mid.tile([P, GROUPS_PER_ROUND, MID_PIX], F32)
-                nc.scalar.copy(out=mid_res[:], in_=mid_sums[rnd][:])
-                groups = slice(rnd * GROUPS_PER_ROUND, (rnd + 1) * GROUPS_PER_ROUND)
-                nc.sync.dma_start(out=out_by_channel[:, groups, mid_first : mid_first + MID_PIX], in_=mid_res[:])
+                n_groups = n_groups_of(rnd)
+                mid_res = mid.tile([P, GROUPS_PER_ROUND, BAND_STORE], F32)
+                nc.scalar.copy(out=mid_res[:, 0:n_groups, :], in_=mid_sums[rnd][:, 0:n_groups, 0:BAND_STORE])
+                nc.scalar.copy(
+                    out=tail_res[:, groups_of(rnd), 0 : end_band - first_tail], in_=mid_sums[rnd][:, 0:n_groups, BAND_STORE:BAND_PIX]
+                )
+                nc.sync.dma_start(
+                    out=out_by_channel[:, groups_of(rnd), BAND_FIRST : BAND_FIRST + BAND_STORE], in_=mid_res[:, 0:n_groups, :]
+                )
 
             units = []
-            for block in EDGE_BLOCKS:
-                for pix in range(block * block_pix, (block + 1) * block_pix):
-                    h, w = pix // W, pix % W
-                    terms = []
-                    for tap in range(TAPS):
-                        source_h, source_w = h + tap // KS - PAD, w + tap % KS - PAD
-                        if 0 <= source_h < H and 0 <= source_w < W:
-                            terms.append((tap, source_h * W + source_w))
-                    n_units = (len(terms) + UNIT_TERMS - 1) // UNIT_TERMS
-                    for u in range(n_units):
-                        part = terms[u * len(terms) // n_units : (u + 1) * len(terms) // n_units]
-                        units.append((pix, part, u == 0, u == n_units - 1))
+            for pix in list(range(BAND_FIRST)) + list(range(end_band, PIX)):
+                h, w = pix // W, pix % W
+                terms = []
+                for tap in range(TAPS):
+                    source_h, source_w = h + tap // KS - PAD, w + tap % KS - PAD
+                    if 0 <= source_h < H and 0 <= source_w < W:
+                        terms.append((tap, source_h * W + source_w))
+                n_units = (len(terms) + UNIT_TERMS - 1) // UNIT_TERMS
+                for u in range(n_units):
+                    part = terms[u * len(terms) // n_units : (u + 1) * len(terms) // n_units]
+                    units.append((pix, part, u == 0, u == n_units - 1))
+            n_units = len(units)
             made = {}
             quad_sums = {}
-            block_res = {}
 
             def counts(u):
                 n = len(units[u][1])
@@ -419,13 +424,15 @@ def tile_involution_k_kernel(tc, x, w_reduce, b_reduce, w_span, b_span, out):
                 n_fused = round(FUSED_SHARE * n)
                 return n_scalar, n - n_scalar - n_fused, n_fused
 
+            most_made = max([counts(u)[0] + counts(u)[1] for u in range(n_units)])
+
             def make_products(u):
                 pix, terms = units[u][0], units[u][1]
                 n_scalar, n_vector, n_fused = counts(u)
-                made[u] = prods.tile([P, UNIT_TERMS, CH], F32, name="made")
+                made[u] = prods.tile([P, most_made, CH], F32, name="made")
                 for k in range(n_scalar + n_vector):
                     tap, source = terms[k]
-                    weight = prob[:, tap, pix : pix + 1]
+                    weight = weights[:, pix, tap : tap + 1]
                     if k < n_scalar:
                         nc.scalar.activation(out=made[u][:, k, :], in_=x_t[:, source, :], func=ACT.Copy, scale=weight)
                     else:
@@ -440,18 +447,23 @@ def tile_involution_k_kernel(tc, x, w_reduce, b_reduce, w_span, b_span, out):
                     tap, source = terms[n_scalar + n_vector + k]
                     mine = made[u][:, k, :]
                     nc.vector.scalar_tensor_tensor(
-                        out=mine, in0=x_t[:, source, :], scalar=prob[:, tap, pix : pix + 1], in1=mine, op0=ALU.mult, op1=ALU.add
+                        out=mine,
+                        in0=x_t[:, source, :],
+                        scalar=weights[:, pix, tap : tap + 1],
+                        in1=mine,
+                        op0=ALU.mult,
+                        op1=ALU.add,
                     )
 
             def sum_products(u):
                 pix, first, last = units[u][0], units[u][2], units[u][3]
-                n_scalar, n_vector, n_fused = counts(u)
-                n_made = n_scalar + n_vector
-                if first and pix % QUAD == 0:
-                    quad_sums[pix // QUAD] = quads.tile([P, QUAD, G], F32, name="quad_sums")
+                n_made = counts(u)[0] + counts(u)[1]
+                quad = pix // QUAD
+                if first and (pix % QUAD == 0 or pix == end_band):
+                    quad_sums[quad] = quads.tile([P, QUAD, G], F32, name="quad_sums")
                 for k in range(n_made):
                     nc.tensor.matmul(
-                        out=quad_sums[pix // QUAD][:, pix % QUAD, :],
+                        out=quad_sums[quad][:, pix % QUAD, :],
                         lhsT=made[u][:, k, :],
                         rhs=ident[:],
                         is_transpose=True,
@@ -459,22 +471,41 @@ def tile_involution_k_kernel(tc, x, w_reduce, b_reduce, w_span, b_span, out):
                         stop=(last and k == n_made - 1),
                     )
 
-            def store_quad(quad):
-                block = quad * QUAD // block_pix
-                if quad * QUAD % block_pix == 0:
-                    block_res[block] = ress.tile([P, G, block_pix], F32, name="block_res")
-                first = quad * QUAD - block * block_pix
+            def finish_quad(quad):
+                first_k = end_band % QUAD if quad == end_band // QUAD else 0
+                first_pix = quad * QUAD
+                res = head_res if first_pix < BLOCK_PIX else tail_res
+                at = first_pix % BLOCK_PIX
                 nc.scalar.copy(
-                    out=block_res[block][:, :, first : first + QUAD], in_=quad_sums[quad][:].rearrange("p k g -> p g k")
+                    out=res[:, :, at + first_k : at + QUAD], in_=quad_sums[quad][:, first_k:QUAD, :].rearrange("p k g -> p g k")
                 )
-                if first + QUAD == block_pix:
-                    for first_g in range(0, G, RES_GROUPS):
-                        groups = slice(first_g, first_g + RES_GROUPS)
-                        nc.sync.dma_start(
-                            out=out_by_channel[:, groups, block * block_pix : (block + 1) * block_pix],
-                            in_=block_res[block][:, groups, :],
-                        )
 
+            def store_block(res, first_pix):
+                for first_g in range(0, G, RES_GROUPS):
+                    groups = slice(first_g, first_g + RES_GROUPS)
+                    nc.sync.dma_start(out=out_by_channel[:, groups, first_pix : first_pix + BLOCK_PIX], in_=res[:, groups, :])
+
+            n_pieces = CH // X_PIECE
+            find_top(0, BAND_FIRST)
+            for pix in range(BAND_FIRST):
+                exponentials(pix)
+            find_top(BAND_FIRST, end_band)
+            find_top(end_band, PIX)
+            normalise(0, BAND_FIRST)
+            for piece in range(n_pieces):
+                gather_channels(nc.vector.tensor_copy, 0, BLOCK_PIX // W + PAD, piece)
+            for quad in range(n_band_quads):
+                part = range(quad * QUAD, min(BAND_PIX, (quad + 1) * QUAD))
+                for m in part:
+                    exponentials(BAND_FIRST + m)
+                pixels = slice(BAND_FIRST + part[0], BAND_FIRST + part[-1] + 1)
+                nc.vector.reciprocal(out=total[:, pixels], in_=total[:, pixels])
+                for m in part:
+                    spread_weights(m)
+                flip_spread(quad)
+                if quad >= 1:
+                    copy_band(quad - 1)
+            copy_band(n_band_quads - 1)
             load_chan(0)
             load_chan(1)
             flip_lead = GROUPS_PER_ROUND + 2
@@ -482,23 +513,31 @@ def tile_involution_k_kernel(tc, x, w_reduce, b_reduce, w_span, b_span, out):
                 flip_chan(group)
             copy_source(0)
             group = 0
-            n_units = len(units)
             for u in range(n_units + 1):
                 if u < n_units:
                     make_products(u)
-                if 1 <= u:
+                if u % 4 == 3 and u // 4 < n_pieces:
+                    gather_channels(nc.scalar.copy, first_tail // W - PAD, H, u // 4)
+                if 20 <= u < 20 + PIX - end_band:
+                    exponentials(end_band + u - 20)
+                if u == 21 + PIX - end_band:
+                    normalise(end_band, PIX)
+                if u >= 1:
                     fuse_products(u - 1)
                     sum_products(u - 1)
                     while group < G and group * n_units < u * G:
                         if group + flip_lead < G:
                             flip_chan(group + flip_lead)
-                        if group % GROUPS_PER_ROUND == GROUPS_PER_ROUND - 1 and group + 1 < G:
+                        if (group + 1) % GROUPS_PER_ROUND == 0 and group + 1 < G:
                             copy_source((group + 1) // GROUPS_PER_ROUND)
                         multiply_band(group)
                         if group % GROUPS_PER_ROUND == 1 and group > GROUPS_PER_ROUND:
                             store_band(group // GROUPS_PER_ROUND - 1)
                         group += 1
                 if u >= 2 and units[u - 2][3] and units[u - 2][0] % QUAD == QUAD - 1:
-                    store_quad(units[u - 2][0] // QUAD)
-            store_quad(units[n_units - 1][0] // QUAD)
+                    finish_quad(units[u - 2][0] // QUAD)
+                    if units[u - 2][0] == BLOCK_PIX - 1:
+                        store_block(head_res, 0)
             store_band(n_rounds - 1)
+            finish_quad(PIX // QUAD - 1)
+            store_block(tail_res, first_tail)

@@ -34,7 +34,7 @@ BAND_STORE = 64
 TAP_PITCH = 52
 QUAD = 4
 UNIT_TERMS = 16
-SCALAR_SHARE, FUSED_SHARE = 0.34, 0.36
+SCALAR_SHARE, FUSED_SHARE = 0.38, 0.48
 GROUPS_PER_ROUND = 7
 
 FLOPS = 2 * R * C * PIX + 2 * TAPS * G * R * PIX + 2 * C * PIX * TAPS

@@ -20,22 +20,30 @@ K_PASS = 4 * P
 PASSES = C // K_PASS
 CHUNK_PASSES = 8
 CHUNKS = PASSES // CHUNK_PASSES
+X_LAG = 3
 X_CHUNK_PASSES = 4
 R_BLOCKS = R // P
 SPAN_LOAD_TAPS = 8
 SPAN_BATCH = 4
-W_BUFS, X_BUFS, SPAN_BUFS = 4, 4, 2
+W_BUFS, X_BUFS = 5, 4
 BLOCK_PIX = 32
 X_PIECE = 32
-RES_GROUPS = 32
+RES_GROUPS = 8
 BAND_FIRST, BAND_PIX = 32, 70
 BAND_PITCH = 72
 BAND_STORE = 64
 TAP_PITCH = 52
 QUAD = 4
-UNIT_TERMS = 16
-SCALAR_SHARE, FUSED_SHARE = 0.38, 0.48
+FINISH_DELAY = 4
 GROUPS_PER_ROUND = 7
+LATE_FIRST = 9 * GROUPS_PER_ROUND
+HEAD_STORE_STEP = 3
+TAIL_GATHER_STEP, TAIL_EXP_STEP = 16, 2
+BAND_LAG = 2
+FLIP_LEAD = GROUPS_PER_ROUND + 4
+STORE_LAG = 3
+UNIT_TERMS = 10
+EARLY_SHARES, LATE_SHARES = (0.4, 0.1), (0.38, 0.32)
 
 FLOPS = 2 * R * C * PIX + 2 * TAPS * G * R * PIX + 2 * C * PIX * TAPS
 
@@ -56,7 +64,7 @@ def tile_involution_k_kernel(tc, x, w_reduce, b_reduce, w_span, b_span, out):
         ident_bf = const.tile([P, P], BF16)
         make_identity(nc, ident_bf[:])
 
-        x_group = keep.tile([P, CH, PIX], BF16)
+        x_group = keep.tile([P, CH, PIX], BF16, tag="x_late")
         x_t = keep.tile([P, PIX, CH], BF16)
         weights = keep.tile([P, PIX, TAP_PITCH], F32)
         top = keep.tile([P, PIX], F32)
@@ -78,13 +86,13 @@ def tile_involution_k_kernel(tc, x, w_reduce, b_reduce, w_span, b_span, out):
             chans = slice(piece * X_PIECE, (piece + 1) * X_PIECE)
             copy(out=x_t[:, pixels, chans], in_=x_group[:, chans, pixels].rearrange("p c s -> p s c"))
 
-        with tc.tile_pool(name="codes", bufs=1) as codes, tc.tile_pool(name="sload", bufs=SPAN_BUFS) as sload, tc.tile_pool(
-            name="sstage", bufs=2
-        ) as sstage, tc.tile_pool(name="scodes", bufs=3) as scodes, tc.tile_pool(name="xload", bufs=X_BUFS) as xload, tc.tile_pool(
-            name="xstage", bufs=2
-        ) as xstage, tc.tile_pool(name="wload", bufs=W_BUFS) as wload, tc.tile_pool(name="wstage", bufs=2) as wstage, tc.psum_pool(
-            name="flip", bufs=4
-        ) as flip, tc.psum_pool(name="sums", bufs=4) as sums, tc.manual_schedule():
+        with tc.tile_pool(name="codes", bufs=1) as codes, tc.tile_pool(name="sstage", bufs=2) as sstage, tc.tile_pool(
+            name="scodes", bufs=3
+        ) as scodes, tc.tile_pool(name="xload", bufs=X_BUFS) as xload, tc.tile_pool(name="xstage", bufs=2) as xstage, tc.tile_pool(
+            name="wload", bufs=W_BUFS
+        ) as wload, tc.tile_pool(name="wstage", bufs=2) as wstage, tc.psum_pool(name="flip", bufs=4) as flip, tc.psum_pool(
+            name="sums", bufs=4
+        ) as sums, tc.manual_schedule():
 
             x_codes = codes.tile([P, PASSES * PIX], U32, align_bytes=64)
             x_scales = codes.tile([P, PASSES * PIX], U8, align_bytes=64)
@@ -102,8 +110,6 @@ def tile_involution_k_kernel(tc, x, w_reduce, b_reduce, w_span, b_span, out):
             def regroup_x(chunk):
                 x_grouped[chunk] = xstage.tile([P, X_CHUNK_PASSES, PIX, 4], BF16, name="x_grouped", align_bytes=64)
                 nc.vector.tensor_copy(out=x_grouped[chunk][:], in_=x_raw[chunk][:].rearrange("p q t s -> p q s t"))
-                if chunk + X_BUFS < n_x_chunks:
-                    load_x(chunk + X_BUFS)
 
             def quantise_x(chunk):
                 cols = slice(chunk * X_CHUNK_PASSES * PIX, (chunk + 1) * X_CHUNK_PASSES * PIX)
@@ -115,18 +121,32 @@ def tile_involution_k_kernel(tc, x, w_reduce, b_reduce, w_span, b_span, out):
 
             n_steps = CHUNKS * R_BLOCKS
             red_sums = [sums.tile([P, PIX], F32, name="red_sums%d" % blk, tag="sums") for blk in range(R_BLOCKS)]
+            n_span_loads = (TAPS + SPAN_LOAD_TAPS - 1) // SPAN_LOAD_TAPS
             w_raw = {}
+            span_raw = {}
             w_grouped = {}
             w_codes = {}
             w_scales = {}
 
             def load_w(step):
                 chunk, blk = step // R_BLOCKS, step % R_BLOCKS
-                w_raw[step] = wload.tile([P, CHUNK_PASSES * K_PASS], BF16, name="w_raw")
+                w_raw[step] = wload.tile([P, CHUNK_PASSES * K_PASS], BF16, name="w_raw", tag="rows")
                 nc.sync.dma_start(
                     out=w_raw[step][:],
                     in_=w_blocks[blk // 2, blk % 2, :, chunk * CHUNK_PASSES * K_PASS : (chunk + 1) * CHUNK_PASSES * K_PASS],
                 )
+
+            def load_span(load):
+                first_tap = load * SPAN_LOAD_TAPS
+                n_load = min(SPAN_LOAD_TAPS, TAPS - first_tap)
+                span_raw[load] = wload.tile([P, SPAN_LOAD_TAPS, R], BF16, name="span_raw", tag="rows")
+                nc.sync.dma_start(out=span_raw[load][:, 0:n_load, :], in_=span_by_group[:, first_tap : first_tap + n_load, :])
+
+            def load_rows(k):
+                if k < n_steps:
+                    load_w(k)
+                elif k < n_steps + n_span_loads:
+                    load_span(k - n_steps)
 
             def flip_w(step):
                 w_words = w_raw[step][:].bitcast(F32)
@@ -141,8 +161,7 @@ def tile_involution_k_kernel(tc, x, w_reduce, b_reduce, w_span, b_span, out):
                     copy_out(
                         out=w_grouped[step][:, 2 * pair : 2 * pair + 2, :, :], in_=w_flip[:].rearrange("p q u r -> p q r u")
                     )
-                if step + W_BUFS < n_steps:
-                    load_w(step + W_BUFS)
+                load_rows(step + W_BUFS)
 
             def quantise_w(step):
                 w_codes[step] = wstage.tile([P, CHUNK_PASSES * P], U32, name="w_codes", align_bytes=64)
@@ -168,26 +187,29 @@ def tile_involution_k_kernel(tc, x, w_reduce, b_reduce, w_span, b_span, out):
                     )
 
             x_ahead = CHUNK_PASSES // X_CHUNK_PASSES
-            for chunk in range(x_ahead):
-                load_x(chunk)
-            for step in range(W_BUFS):
+            load_w(0)
+            load_x(0)
+            load_w(1)
+            load_x(1)
+            for step in range(2, W_BUFS):
                 load_w(step)
-            for chunk in range(x_ahead, X_BUFS):
-                load_x(chunk)
-            for chunk in range(x_ahead):
-                regroup_x(chunk)
-            for chunk in range(x_ahead):
-                quantise_x(chunk)
             for n in range(n_steps + 2):
-                x_chunk = n // 2 + x_ahead
-                with_x = n % 2 == 0 and x_chunk < n_x_chunks
+                x_chunk = (n - X_LAG) // 2 + x_ahead
+                with_x = n >= X_LAG and (n - X_LAG) % 2 == 0 and x_chunk < n_x_chunks
+                if n % 2 == 0 and n // 2 + x_ahead < n_x_chunks:
+                    load_x(n // 2 + x_ahead)
                 if n < n_steps:
                     flip_w(n)
-                if with_x:
-                    regroup_x(x_chunk)
+                if n == 0:
+                    for chunk in range(x_ahead):
+                        regroup_x(chunk)
                 if 1 <= n <= n_steps:
                     quantise_w(n - 1)
+                if n == 0:
+                    for chunk in range(x_ahead):
+                        quantise_x(chunk)
                 if with_x:
+                    regroup_x(x_chunk)
                     quantise_x(x_chunk)
                 if n >= 2:
                     multiply_w(n - 2)
@@ -203,9 +225,7 @@ def tile_involution_k_kernel(tc, x, w_reduce, b_reduce, w_span, b_span, out):
                 out=red_codes[:].bitcast(FP8X4), scales=red_scales[:], in_=red_grouped[:].rearrange("p s t -> p (s t)")
             )
 
-            n_span_loads = (TAPS + SPAN_LOAD_TAPS - 1) // SPAN_LOAD_TAPS
             n_batches = (TAPS + SPAN_BATCH - 1) // SPAN_BATCH
-            span_raw = {}
             span_grouped = {}
             span_codes = {}
             span_scales = {}
@@ -213,12 +233,6 @@ def tile_involution_k_kernel(tc, x, w_reduce, b_reduce, w_span, b_span, out):
 
             def taps_of(batch):
                 return min(SPAN_BATCH, TAPS - batch * SPAN_BATCH)
-
-            def load_span(load):
-                first_tap = load * SPAN_LOAD_TAPS
-                n_load = min(SPAN_LOAD_TAPS, TAPS - first_tap)
-                span_raw[load] = sload.tile([P, SPAN_LOAD_TAPS, R], BF16, name="span_raw")
-                nc.sync.dma_start(out=span_raw[load][:, 0:n_load, :], in_=span_by_group[:, first_tap : first_tap + n_load, :])
 
             def flip_span(batch):
                 span_grouped[batch] = sstage.tile([P, SPAN_BATCH, G, 2], F32, name="span_grouped", align_bytes=64)
@@ -235,8 +249,8 @@ def tile_involution_k_kernel(tc, x, w_reduce, b_reduce, w_span, b_span, out):
                         in_=span_flip[:, 0:n_pair, :, :].rearrange("p k u g -> p k g u"),
                     )
                 end_tap = batch * SPAN_BATCH + taps_of(batch)
-                if end_tap % SPAN_LOAD_TAPS == 0 and end_tap // SPAN_LOAD_TAPS - 1 + SPAN_BUFS < n_span_loads:
-                    load_span(end_tap // SPAN_LOAD_TAPS - 1 + SPAN_BUFS)
+                if end_tap % SPAN_LOAD_TAPS == 0:
+                    load_rows(n_steps + end_tap // SPAN_LOAD_TAPS - 1 + W_BUFS)
 
             def quantise_span(batch):
                 n_taps = taps_of(batch)
@@ -271,8 +285,6 @@ def tile_involution_k_kernel(tc, x, w_reduce, b_reduce, w_span, b_span, out):
                     op=ALU.add,
                 )
 
-            for load in range(SPAN_BUFS):
-                load_span(load)
             for n in range(n_batches + 3):
                 if n < n_batches:
                     flip_span(n)
@@ -289,6 +301,7 @@ def tile_involution_k_kernel(tc, x, w_reduce, b_reduce, w_span, b_span, out):
 
         end_band = BAND_FIRST + BAND_PIX
         first_tail = PIX - BLOCK_PIX
+        n_band_quads = (BAND_PIX + QUAD - 1) // QUAD
 
         def find_top(first_pix, end_pix):
             part = slice(first_pix, end_pix)
@@ -315,8 +328,8 @@ def tile_involution_k_kernel(tc, x, w_reduce, b_reduce, w_span, b_span, out):
             name="flip2", bufs=2
         ) as flip2, tc.psum_pool(name="xflip", bufs=2) as xflip, tc.psum_pool(name="osum", bufs=2) as osum, tc.psum_pool(
             name="quads", bufs=2
-        ) as quads, tc.tile_pool(name="prods", bufs=4) as prods, tc.tile_pool(name="res", bufs=1) as ress, tc.manual_schedule():
-            spread = bands.tile([P, BAND_PIX, PIX], F32)
+        ) as quads, tc.tile_pool(name="prods", bufs=6) as prods, tc.tile_pool(name="res", bufs=1) as ress, tc.manual_schedule():
+            spread = bands.tile([P, BAND_PIX, PIX], F32, tag="wide")
             nc.gpsimd.memset(spread[:], 0.0)
             spread_hw = spread[:].rearrange("p m (h w) -> p m h w", w=W)
             band = bands.tile([P, G, BAND_PITCH], F32)
@@ -335,8 +348,6 @@ def tile_involution_k_kernel(tc, x, w_reduce, b_reduce, w_span, b_span, out):
                     op0=ALU.mult,
                 )
 
-            n_band_quads = (BAND_PIX + QUAD - 1) // QUAD
-
             def flip_spread(quad):
                 spread_flip[quad] = flip2.tile([P, QUAD, G], F32, name="spread_flip")
                 for k in range(min(QUAD, BAND_PIX - quad * QUAD)):
@@ -344,7 +355,8 @@ def tile_involution_k_kernel(tc, x, w_reduce, b_reduce, w_span, b_span, out):
 
             def copy_band(quad):
                 n_pix = min(QUAD, BAND_PIX - quad * QUAD)
-                nc.scalar.copy(
+                copy_out = nc.vector.tensor_copy if quad % 2 else nc.scalar.copy
+                copy_out(
                     out=band[:, :, quad * QUAD : quad * QUAD + n_pix],
                     in_=spread_flip[quad][:, 0:n_pix, :].rearrange("p k g -> p g k"),
                 )
@@ -355,7 +367,8 @@ def tile_involution_k_kernel(tc, x, w_reduce, b_reduce, w_span, b_span, out):
             x_source = {}
             mid_sums = {}
             head_res = ress.tile([P, G, BLOCK_PIX], F32)
-            tail_res = ress.tile([P, G, BLOCK_PIX], F32)
+            tail_res = ress.tile([P, LATE_FIRST, BLOCK_PIX], F32)
+            late_res = []
 
             def groups_of(rnd):
                 return slice(rnd * GROUPS_PER_ROUND, min(G, (rnd + 1) * GROUPS_PER_ROUND))
@@ -367,17 +380,24 @@ def tile_involution_k_kernel(tc, x, w_reduce, b_reduce, w_span, b_span, out):
                 x_chan[rnd] = mid.tile([P, GROUPS_PER_ROUND, PIX], BF16, name="x_chan")
                 nc.sync.dma_start(out=x_chan[rnd][:, 0 : n_groups_of(rnd), :], in_=x_by_channel[:, groups_of(rnd), :])
 
+            def load_late():
+                x_late = keep.tile([P, G - LATE_FIRST, PIX], BF16, tag="x_late")
+                nc.sync.dma_start(out=x_late[:], in_=x_by_channel[:, LATE_FIRST:G, :])
+                for rnd in range(LATE_FIRST // GROUPS_PER_ROUND, n_rounds):
+                    x_chan[rnd] = x_late[:, rnd * GROUPS_PER_ROUND - LATE_FIRST : groups_of(rnd).stop - LATE_FIRST, :]
+
             def flip_chan(group):
                 rnd, k = group // GROUPS_PER_ROUND, group % GROUPS_PER_ROUND
                 if k == 0:
                     x_flip[rnd] = xflip.tile([P, GROUPS_PER_ROUND, CH], BF16, name="x_flip")
                 nc.tensor.transpose(x_flip[rnd][:, k, :], x_chan[rnd][:, k, :], ident_bf[:])
-                if k == n_groups_of(rnd) - 1 and rnd + 2 < n_rounds:
+                if k == GROUPS_PER_ROUND - 1 and (rnd + 2) * GROUPS_PER_ROUND < LATE_FIRST:
                     load_chan(rnd + 2)
 
             def copy_source(rnd):
                 x_source[rnd] = mid.tile([P, GROUPS_PER_ROUND, CH], F32, name="x_source")
-                nc.scalar.copy(out=x_source[rnd][:, 0 : n_groups_of(rnd), :], in_=x_flip[rnd][:, 0 : n_groups_of(rnd), :])
+                copy_out = nc.vector.tensor_copy if rnd % 2 and rnd > LATE_FIRST // GROUPS_PER_ROUND else nc.scalar.copy
+                copy_out(out=x_source[rnd][:, 0 : n_groups_of(rnd), :], in_=x_flip[rnd][:, 0 : n_groups_of(rnd), :])
 
             def multiply_band(group):
                 rnd, k = group // GROUPS_PER_ROUND, group % GROUPS_PER_ROUND
@@ -393,14 +413,20 @@ def tile_involution_k_kernel(tc, x, w_reduce, b_reduce, w_span, b_span, out):
 
             def store_band(rnd):
                 n_groups = n_groups_of(rnd)
+                sums_of = mid_sums[rnd][:, 0:n_groups, :]
                 mid_res = mid.tile([P, GROUPS_PER_ROUND, BAND_STORE], F32)
-                nc.scalar.copy(out=mid_res[:, 0:n_groups, :], in_=mid_sums[rnd][:, 0:n_groups, 0:BAND_STORE])
-                nc.scalar.copy(
-                    out=tail_res[:, groups_of(rnd), 0 : end_band - first_tail], in_=mid_sums[rnd][:, 0:n_groups, BAND_STORE:BAND_PIX]
-                )
+                nc.scalar.copy(out=mid_res[:, 0:n_groups, :], in_=sums_of[:, :, 0:BAND_STORE])
+                nc.scalar.copy(out=tail_res[:, groups_of(rnd), 0 : end_band - first_tail], in_=sums_of[:, :, BAND_STORE:BAND_PIX])
                 nc.sync.dma_start(
                     out=out_by_channel[:, groups_of(rnd), BAND_FIRST : BAND_FIRST + BAND_STORE], in_=mid_res[:, 0:n_groups, :]
                 )
+
+            def store_late(rnd):
+                groups = groups_of(rnd)
+                mine = late_res[0][:, groups.start - LATE_FIRST : groups.stop - LATE_FIRST, :]
+                copy_out = nc.vector.tensor_copy if rnd % 2 else nc.scalar.copy
+                copy_out(out=mine[:, :, 0:BAND_PIX], in_=mid_sums[rnd][:, 0 : n_groups_of(rnd), :])
+                nc.sync.dma_start(out=out_by_channel[:, groups, BAND_FIRST:PIX], in_=mine)
 
             units = []
             for pix in list(range(BAND_FIRST)) + list(range(end_band, PIX)):
@@ -415,20 +441,26 @@ def tile_involution_k_kernel(tc, x, w_reduce, b_reduce, w_span, b_span, out):
                     part = terms[u * len(terms) // n_units : (u + 1) * len(terms) // n_units]
                     units.append((pix, part, u == 0, u == n_units - 1))
             n_units = len(units)
+            band_unit = n_band_quads + BAND_LAG + 1
             made = {}
             quad_sums = {}
 
-            def counts(u):
+            split = []
+            done_terms = 0
+            for u in range(n_units):
+                scalar_share, fused_share = EARLY_SHARES if u < band_unit else LATE_SHARES
                 n = len(units[u][1])
-                n_scalar = round(SCALAR_SHARE * n)
-                n_fused = round(FUSED_SHARE * n)
-                return n_scalar, n - n_scalar - n_fused, n_fused
+                n_scalar = int(scalar_share * (done_terms + n)) - int(scalar_share * done_terms)
+                n_fused = min(n - n_scalar, int(fused_share * (done_terms + n)) - int(fused_share * done_terms))
+                n_fused = min(n_fused, n - n_fused)
+                split.append((n_scalar, n - n_scalar - n_fused, n_fused))
+                done_terms += n
 
-            most_made = max([counts(u)[0] + counts(u)[1] for u in range(n_units)])
+            most_made = max([split[u][0] + split[u][1] for u in range(n_units)])
 
             def make_products(u):
                 pix, terms = units[u][0], units[u][1]
-                n_scalar, n_vector, n_fused = counts(u)
+                n_scalar, n_vector, n_fused = split[u]
                 made[u] = prods.tile([P, most_made, CH], F32, name="made")
                 for k in range(n_scalar + n_vector):
                     tap, source = terms[k]
@@ -442,7 +474,7 @@ def tile_involution_k_kernel(tc, x, w_reduce, b_reduce, w_span, b_span, out):
 
             def fuse_products(u):
                 pix, terms = units[u][0], units[u][1]
-                n_scalar, n_vector, n_fused = counts(u)
+                n_scalar, n_vector, n_fused = split[u]
                 for k in range(n_fused):
                     tap, source = terms[n_scalar + n_vector + k]
                     mine = made[u][:, k, :]
@@ -457,7 +489,7 @@ def tile_involution_k_kernel(tc, x, w_reduce, b_reduce, w_span, b_span, out):
 
             def sum_products(u):
                 pix, first, last = units[u][0], units[u][2], units[u][3]
-                n_made = counts(u)[0] + counts(u)[1]
+                n_made = split[u][0] + split[u][1]
                 quad = pix // QUAD
                 if first and (pix % QUAD == 0 or pix == end_band):
                     quad_sums[quad] = quads.tile([P, QUAD, G], F32, name="quad_sums")
@@ -473,71 +505,95 @@ def tile_involution_k_kernel(tc, x, w_reduce, b_reduce, w_span, b_span, out):
 
             def finish_quad(quad):
                 first_k = end_band % QUAD if quad == end_band // QUAD else 0
-                first_pix = quad * QUAD
-                res = head_res if first_pix < BLOCK_PIX else tail_res
-                at = first_pix % BLOCK_PIX
-                nc.scalar.copy(
-                    out=res[:, :, at + first_k : at + QUAD], in_=quad_sums[quad][:, first_k:QUAD, :].rearrange("p k g -> p g k")
-                )
+                sums_of = quad_sums[quad][:, first_k:QUAD, :].rearrange("p k g -> p g k")
+                pixels = [quad * QUAD + first_k, (quad + 1) * QUAD]
+                if pixels[0] < BLOCK_PIX:
+                    nc.scalar.copy(out=head_res[:, :, pixels[0] : pixels[1]], in_=sums_of)
+                else:
+                    if not late_res:
+                        late_res.append(bands.tile([P, G - LATE_FIRST, PIX - BAND_FIRST], F32, name="late_res", tag="wide"))
+                    nc.scalar.copy(
+                        out=tail_res[:, :, pixels[0] - first_tail : pixels[1] - first_tail], in_=sums_of[:, 0:LATE_FIRST, :]
+                    )
+                    nc.scalar.copy(
+                        out=late_res[0][:, :, pixels[0] - BAND_FIRST : pixels[1] - BAND_FIRST], in_=sums_of[:, LATE_FIRST:G, :]
+                    )
 
-            def store_block(res, first_pix):
-                for first_g in range(0, G, RES_GROUPS):
-                    groups = slice(first_g, first_g + RES_GROUPS)
-                    nc.sync.dma_start(out=out_by_channel[:, groups, first_pix : first_pix + BLOCK_PIX], in_=res[:, groups, :])
+            def store_block(res, first_pix, groups):
+                nc.sync.dma_start(out=out_by_channel[:, groups, first_pix : first_pix + BLOCK_PIX], in_=res[:, groups, :])
 
             n_pieces = CH // X_PIECE
             find_top(0, BAND_FIRST)
             for pix in range(BAND_FIRST):
                 exponentials(pix)
             find_top(BAND_FIRST, end_band)
-            find_top(end_band, PIX)
+            for pix in range(BAND_FIRST, end_band):
+                exponentials(pix)
             normalise(0, BAND_FIRST)
             for piece in range(n_pieces):
                 gather_channels(nc.vector.tensor_copy, 0, BLOCK_PIX // W + PAD, piece)
-            for quad in range(n_band_quads):
-                part = range(quad * QUAD, min(BAND_PIX, (quad + 1) * QUAD))
-                for m in part:
-                    exponentials(BAND_FIRST + m)
-                pixels = slice(BAND_FIRST + part[0], BAND_FIRST + part[-1] + 1)
-                nc.vector.reciprocal(out=total[:, pixels], in_=total[:, pixels])
-                for m in part:
-                    spread_weights(m)
-                flip_spread(quad)
-                if quad >= 1:
-                    copy_band(quad - 1)
-            copy_band(n_band_quads - 1)
+            find_top(end_band, PIX)
+            nc.vector.reciprocal(out=total[:, BAND_FIRST:end_band], in_=total[:, BAND_FIRST:end_band])
             load_chan(0)
             load_chan(1)
-            flip_lead = GROUPS_PER_ROUND + 2
-            for group in range(flip_lead):
-                flip_chan(group)
-            copy_source(0)
             group = 0
+            head_done = -1
+
+            def band_step(group):
+                if group + FLIP_LEAD < G:
+                    flip_chan(group + FLIP_LEAD)
+                if (group + 2) % GROUPS_PER_ROUND == 0 and group + 2 < G:
+                    copy_source((group + 2) // GROUPS_PER_ROUND)
+                multiply_band(group)
+                rnd = group // GROUPS_PER_ROUND - 1
+                if group % GROUPS_PER_ROUND == STORE_LAG and rnd >= 0:
+                    if rnd * GROUPS_PER_ROUND < LATE_FIRST:
+                        store_band(rnd)
+                    else:
+                        store_late(rnd)
+
             for u in range(n_units + 1):
                 if u < n_units:
                     make_products(u)
-                if u % 4 == 3 and u // 4 < n_pieces:
-                    gather_channels(nc.scalar.copy, first_tail // W - PAD, H, u // 4)
-                if 20 <= u < 20 + PIX - end_band:
-                    exponentials(end_band + u - 20)
-                if u == 21 + PIX - end_band:
+                if u < n_band_quads:
+                    for m in range(u * QUAD, min(BAND_PIX, (u + 1) * QUAD)):
+                        spread_weights(m)
+                    flip_spread(u)
+                if BAND_LAG <= u < n_band_quads + BAND_LAG:
+                    copy_band(u - BAND_LAG)
+                if u == n_band_quads:
+                    for k in range(FLIP_LEAD):
+                        flip_chan(k)
+                if u == band_unit - 1:
+                    copy_source(0)
+                if u % TAIL_GATHER_STEP == 0 and u // TAIL_GATHER_STEP <= n_pieces and u:
+                    gather_channels(nc.scalar.copy, first_tail // W - PAD, H, u // TAIL_GATHER_STEP - 1)
+                if u == TAIL_GATHER_STEP * n_pieces + 2:
+                    load_late()
+                pix = end_band + (u - band_unit) // TAIL_EXP_STEP
+                if end_band <= pix < PIX and (u - band_unit) % TAIL_EXP_STEP == 0:
+                    exponentials(pix)
+                if pix == PIX and (u - band_unit) % TAIL_EXP_STEP == 1:
                     normalise(end_band, PIX)
                 if u >= 1:
                     fuse_products(u - 1)
                     sum_products(u - 1)
-                    while group < G and group * n_units < u * G:
-                        if group + flip_lead < G:
-                            flip_chan(group + flip_lead)
-                        if (group + 1) % GROUPS_PER_ROUND == 0 and group + 1 < G:
-                            copy_source((group + 1) // GROUPS_PER_ROUND)
-                        multiply_band(group)
-                        if group % GROUPS_PER_ROUND == 1 and group > GROUPS_PER_ROUND:
-                            store_band(group // GROUPS_PER_ROUND - 1)
+                    while group < LATE_FIRST and group * (n_units - band_unit) < (u - band_unit) * LATE_FIRST:
+                        band_step(group)
                         group += 1
-                if u >= 2 and units[u - 2][3] and units[u - 2][0] % QUAD == QUAD - 1:
-                    finish_quad(units[u - 2][0] // QUAD)
-                    if units[u - 2][0] == BLOCK_PIX - 1:
-                        store_block(head_res, 0)
-            store_band(n_rounds - 1)
+                done = u - FINISH_DELAY
+                if done >= 0 and units[done][3] and units[done][0] % QUAD == QUAD - 1:
+                    finish_quad(units[done][0] // QUAD)
+                    if units[done][0] == BLOCK_PIX - 1:
+                        head_done = u
+                if head_done >= 0 and (u - head_done) % HEAD_STORE_STEP == 0 and (u - head_done) // HEAD_STORE_STEP < G // RES_GROUPS:
+                    first_g = (u - head_done) // HEAD_STORE_STEP * RES_GROUPS
+                    store_block(head_res, 0, slice(first_g, first_g + RES_GROUPS))
             finish_quad(PIX // QUAD - 1)
-            store_block(tail_res, first_tail)
+            for group in range(LATE_FIRST, G):
+                band_step(group)
+                if group == LATE_FIRST + STORE_LAG:
+                    for first_g in range(0, LATE_FIRST, GROUPS_PER_ROUND * 3):
+                        store_block(tail_res, first_tail, slice(first_g, first_g + GROUPS_PER_ROUND * 3))
+            for rnd in range(n_rounds - 2, n_rounds):
+                store_late(rnd)

import concourse.mybir as mybir
from concourse.masks import make_identity

F32 = mybir.dt.float32
BF16 = mybir.dt.bfloat16
U32 = mybir.dt.uint32
U8 = mybir.dt.uint8
FP8X4 = mybir.dt.float8_e4m3fn_x4
ALU = mybir.AluOpType
ACT = mybir.ActivationFunctionType
AXIS = mybir.AxisListType

P = 128
C, H, W, R, G, KS = 16384, 16, 8, 512, 128, 7
PIX = H * W
CH = C // G
TAPS = KS * KS
PAD = KS // 2
K_PASS = 4 * P
PASSES = C // K_PASS
CHUNK_PASSES = 8
CHUNKS = PASSES // CHUNK_PASSES
X_LAG = 3
X_CHUNK_PASSES = 4
R_BLOCKS = R // P
SPAN_LOAD_TAPS = 8
SPAN_BATCH = 4
W_BUFS, X_BUFS = 5, 4
BLOCK_PIX = 32
X_PIECE = 32
RES_GROUPS = 8
BAND_FIRST, BAND_PIX = 32, 70
BAND_PITCH = 72
BAND_STORE = 64
TAP_PITCH = 52
QUAD = 4
FINISH_DELAY = 4
GROUPS_PER_ROUND = 7
LATE_FIRST = 9 * GROUPS_PER_ROUND
HEAD_STORE_STEP = 3
TAIL_GATHER_STEP, TAIL_EXP_STEP = 16, 2
BAND_LAG = 2
FLIP_LEAD = GROUPS_PER_ROUND + 4
STORE_LAG = 3
UNIT_TERMS = 10
EARLY_SHARES, LATE_SHARES = (0.4, 0.1), (0.38, 0.32)

FLOPS = 2 * R * C * PIX + 2 * TAPS * G * R * PIX + 2 * C * PIX * TAPS


def tile_involution_k_kernel(tc, x, w_reduce, b_reduce, w_span, b_span, out):
    nc = tc.nc
    x_rows = x.rearrange("b c h w -> (b c) (h w)")
    x_by_pass = x_rows.rearrange("(q u p e) s -> p q u (e s)", q=PASSES, u=2, p=P, e=2)
    x_by_group = x_rows.rearrange("(g c) s -> g c s", c=CH)
    x_by_channel = x_rows.rearrange("(g c) s -> c g s", c=CH)
    out_by_channel = out.rearrange("b (g c) h w -> c g (b h w)", c=CH)
    w_blocks = w_reduce.rearrange("(u p e) c -> u e p c", u=2, p=P, e=2)
    span_by_group = w_span.rearrange("(g t) r -> g t r", t=TAPS)

    with tc.tile_pool(name="const", bufs=1) as const, tc.tile_pool(name="keep", bufs=1) as keep:
        ident = const.tile([P, P], F32)
        make_identity(nc, ident[:])
        ident_bf = const.tile([P, P], BF16)
        make_identity(nc, ident_bf[:])

        x_group = keep.tile([P, CH, PIX], BF16, tag="x_late")
        x_t = keep.tile([P, PIX, CH], BF16)
        weights = keep.tile([P, PIX, TAP_PITCH], F32)
        top = keep.tile([P, PIX], F32)
        total = keep.tile([P, PIX], F32)

        b_red_bf = const.tile([P, R_BLOCKS], BF16)
        nc.scalar.dma_start(
            out=b_red_bf[:].rearrange("p (u e) -> p u e", u=2), in_=b_reduce.rearrange("(u p e) -> p u e", u=2, p=P, e=2)
        )
        b_red = const.tile([P, R_BLOCKS], F32)
        nc.vector.tensor_copy(out=b_red[:], in_=b_red_bf[:])
        b_tap_bf = const.tile([P, TAPS], BF16)
        nc.scalar.dma_start(out=b_tap_bf[:], in_=b_span.rearrange("(g t) -> g t", t=TAPS))
        b_tap = const.tile([P, TAPS], F32)
        nc.vector.tensor_copy(out=b_tap[:], in_=b_tap_bf[:])

        def gather_channels(copy, first_row, end_row, piece):
            pixels = slice(first_row * W, end_row * W)
            chans = slice(piece * X_PIECE, (piece + 1) * X_PIECE)
            copy(out=x_t[:, pixels, chans], in_=x_group[:, chans, pixels].rearrange("p c s -> p s c"))

        with tc.tile_pool(name="codes", bufs=1) as codes, tc.tile_pool(name="sstage", bufs=2) as sstage, tc.tile_pool(
            name="scodes", bufs=3
        ) as scodes, tc.tile_pool(name="xload", bufs=X_BUFS) as xload, tc.tile_pool(name="xstage", bufs=2) as xstage, tc.tile_pool(
            name="wload", bufs=W_BUFS
        ) as wload, tc.tile_pool(name="wstage", bufs=2) as wstage, tc.psum_pool(name="flip", bufs=4) as flip, tc.psum_pool(
            name="sums", bufs=4
        ) as sums, tc.manual_schedule():

            x_codes = codes.tile([P, PASSES * PIX], U32, align_bytes=64)
            x_scales = codes.tile([P, PASSES * PIX], U8, align_bytes=64)
            n_x_chunks = PASSES // X_CHUNK_PASSES
            x_raw = {}
            x_grouped = {}

            def load_x(chunk):
                x_raw[chunk] = xload.tile([P, X_CHUNK_PASSES, 4, PIX], BF16, name="x_raw")
                nc.sync.dma_start(
                    out=x_raw[chunk][:].rearrange("p q (u e) s -> p q u (e s)", u=2),
                    in_=x_by_pass[:, chunk * X_CHUNK_PASSES : (chunk + 1) * X_CHUNK_PASSES],
                )

            def regroup_x(chunk):
                x_grouped[chunk] = xstage.tile([P, X_CHUNK_PASSES, PIX, 4], BF16, name="x_grouped", align_bytes=64)
                nc.vector.tensor_copy(out=x_grouped[chunk][:], in_=x_raw[chunk][:].rearrange("p q t s -> p q s t"))

            def quantise_x(chunk):
                cols = slice(chunk * X_CHUNK_PASSES * PIX, (chunk + 1) * X_CHUNK_PASSES * PIX)
                nc.vector.quantize_mx(
                    out=x_codes[:, cols].bitcast(FP8X4),
                    scales=x_scales[:, cols],
                    in_=x_grouped[chunk][:].rearrange("p q s t -> p (q s t)"),
                )

            n_steps = CHUNKS * R_BLOCKS
            red_sums = [sums.tile([P, PIX], F32, name="red_sums%d" % blk, tag="sums") for blk in range(R_BLOCKS)]
            n_span_loads = (TAPS + SPAN_LOAD_TAPS - 1) // SPAN_LOAD_TAPS
            w_raw = {}
            span_raw = {}
            w_grouped = {}
            w_codes = {}
            w_scales = {}

            def load_w(step):
                chunk, blk = step // R_BLOCKS, step % R_BLOCKS
                w_raw[step] = wload.tile([P, CHUNK_PASSES * K_PASS], BF16, name="w_raw", tag="rows")
                nc.sync.dma_start(
                    out=w_raw[step][:],
                    in_=w_blocks[blk // 2, blk % 2, :, chunk * CHUNK_PASSES * K_PASS : (chunk + 1) * CHUNK_PASSES * K_PASS],
                )

            def load_span(load):
                first_tap = load * SPAN_LOAD_TAPS
                n_load = min(SPAN_LOAD_TAPS, TAPS - first_tap)
                span_raw[load] = wload.tile([P, SPAN_LOAD_TAPS, R], BF16, name="span_raw", tag="rows")
                nc.sync.dma_start(out=span_raw[load][:, 0:n_load, :], in_=span_by_group[:, first_tap : first_tap + n_load, :])

            def load_rows(k):
                if k < n_steps:
                    load_w(k)
                elif k < n_steps + n_span_loads:
                    load_span(k - n_steps)

            def flip_w(step):
                w_words = w_raw[step][:].bitcast(F32)
                w_grouped[step] = wstage.tile([P, CHUNK_PASSES, P, 2], F32, name="w_grouped", align_bytes=64)
                for pair in range(CHUNK_PASSES // 2):
                    w_flip = flip.tile([P, 2, 2, P], F32, tag="flip")
                    for q in range(2):
                        for u in range(2):
                            first = (2 * pair + q) * 2 * P + u * P
                            nc.tensor.transpose(w_flip[:, q, u, :], w_words[:, first : first + P], ident[:])
                    copy_out = nc.vector.tensor_copy if pair == 0 else nc.scalar.copy
                    copy_out(
                        out=w_grouped[step][:, 2 * pair : 2 * pair + 2, :, :], in_=w_flip[:].rearrange("p q u r -> p q r u")
                    )
                load_rows(step + W_BUFS)

            def quantise_w(step):
                w_codes[step] = wstage.tile([P, CHUNK_PASSES * P], U32, name="w_codes", align_bytes=64)
                w_scales[step] = wstage.tile([P, CHUNK_PASSES * P], U8, name="w_scales", align_bytes=64)
                nc.vector.quantize_mx(
                    out=w_codes[step][:].bitcast(FP8X4),
                    scales=w_scales[step][:],
                    in_=w_grouped[step][:].rearrange("p q r u -> p (q r u)").bitcast(BF16),
                )

            def multiply_w(step):
                chunk, blk = step // R_BLOCKS, step % R_BLOCKS
                for q in range(CHUNK_PASSES):
                    k_pass = chunk * CHUNK_PASSES + q
                    nc.tensor.matmul_mx(
                        out=red_sums[blk][:],
                        lhsT=w_codes[step][:, q * P : (q + 1) * P].bitcast(FP8X4),
                        lhsT_scale=w_scales[step][:, q * P : (q + 1) * P],
                        rhs=x_codes[:, k_pass * PIX : (k_pass + 1) * PIX].bitcast(FP8X4),
                        rhs_scale=x_scales[:, k_pass * PIX : (k_pass + 1) * PIX],
                        start=(k_pass == 0),
                        stop=(k_pass == PASSES - 1),
                    )

            x_ahead = CHUNK_PASSES // X_CHUNK_PASSES
            load_w(0)
            load_x(0)
            load_w(1)
            load_x(1)
            for step in range(2, W_BUFS):
                load_w(step)
            for n in range(n_steps + 2):
                x_chunk = (n - X_LAG) // 2 + x_ahead
                with_x = n >= X_LAG and (n - X_LAG) % 2 == 0 and x_chunk < n_x_chunks
                if n % 2 == 0 and n // 2 + x_ahead < n_x_chunks:
                    load_x(n // 2 + x_ahead)
                if n < n_steps:
                    flip_w(n)
                if n == 0:
                    for chunk in range(x_ahead):
                        regroup_x(chunk)
                if 1 <= n <= n_steps:
                    quantise_w(n - 1)
                if n == 0:
                    for chunk in range(x_ahead):
                        quantise_x(chunk)
                if with_x:
                    regroup_x(x_chunk)
                    quantise_x(x_chunk)
                if n >= 2:
                    multiply_w(n - 2)

            red_grouped = codes.tile([P, PIX, R_BLOCKS], BF16, align_bytes=64)
            for blk in range(R_BLOCKS):
                nc.scalar.activation(
                    out=red_grouped[:, :, blk], in_=red_sums[blk][:], func=ACT.Relu, bias=b_red[:, blk : blk + 1], scale=1.0
                )
            red_codes = codes.tile([P, PIX], U32, align_bytes=64)
            red_scales = codes.tile([P, PIX], U8, align_bytes=64)
            nc.vector.quantize_mx(
                out=red_codes[:].bitcast(FP8X4), scales=red_scales[:], in_=red_grouped[:].rearrange("p s t -> p (s t)")
            )

            n_batches = (TAPS + SPAN_BATCH - 1) // SPAN_BATCH
            span_grouped = {}
            span_codes = {}
            span_scales = {}
            kern_sums = {}

            def taps_of(batch):
                return min(SPAN_BATCH, TAPS - batch * SPAN_BATCH)

            def flip_span(batch):
                span_grouped[batch] = sstage.tile([P, SPAN_BATCH, G, 2], F32, name="span_grouped", align_bytes=64)
                for pair in range(0, taps_of(batch), 2):
                    n_pair = min(2, taps_of(batch) - pair)
                    span_flip = flip.tile([P, 2, 2, G], F32, tag="flip")
                    for k in range(n_pair):
                        tap = batch * SPAN_BATCH + pair + k
                        span_words = span_raw[tap // SPAN_LOAD_TAPS][:, tap % SPAN_LOAD_TAPS, :].bitcast(F32)
                        for u in range(2):
                            nc.tensor.transpose(span_flip[:, k, u, :], span_words[:, u * P : (u + 1) * P], ident[:])
                    nc.scalar.copy(
                        out=span_grouped[batch][:, pair : pair + n_pair, :, :],
                        in_=span_flip[:, 0:n_pair, :, :].rearrange("p k u g -> p k g u"),
                    )
                end_tap = batch * SPAN_BATCH + taps_of(batch)
                if end_tap % SPAN_LOAD_TAPS == 0:
                    load_rows(n_steps + end_tap // SPAN_LOAD_TAPS - 1 + W_BUFS)

            def quantise_span(batch):
                n_taps = taps_of(batch)
                span_codes[batch] = scodes.tile([P, SPAN_BATCH * G], U32, name="span_codes", align_bytes=64)
                span_scales[batch] = scodes.tile([P, SPAN_BATCH * G], U8, name="span_scales", align_bytes=64)
                nc.vector.quantize_mx(
                    out=span_codes[batch][:, 0 : n_taps * G].bitcast(FP8X4),
                    scales=span_scales[batch][:, 0 : n_taps * G],
                    in_=span_grouped[batch][:, 0:n_taps, :, :].rearrange("p k g u -> p (k g u)").bitcast(BF16),
                )

            def multiply_span(batch):
                kern_sums[batch] = sums.tile([P, SPAN_BATCH, PIX], F32, name="kern_sums", tag="sums")
                for k in range(taps_of(batch)):
                    nc.tensor.matmul_mx(
                        out=kern_sums[batch][:, k, :],
                        lhsT=span_codes[batch][:, k * G : (k + 1) * G].bitcast(FP8X4),
                        lhsT_scale=span_scales[batch][:, k * G : (k + 1) * G],
                        rhs=red_codes[:].bitcast(FP8X4),
                        rhs_scale=red_scales[:],
                        start=True,
                        stop=True,
                    )

            def add_bias(batch):
                n_taps = taps_of(batch)
                taps = slice(batch * SPAN_BATCH, batch * SPAN_BATCH + n_taps)
                nc.vector.tensor_tensor(
                    out=weights[:, :, taps],
                    in0=kern_sums[batch][:, 0:n_taps, :].rearrange("p k s -> p s k"),
                    in1=b_tap[:, taps].unsqueeze(1).to_broadcast([P, PIX, n_taps]),
                    op=ALU.add,
                )

            for n in range(n_batches + 3):
                if n < n_batches:
                    flip_span(n)
                if 1 <= n <= n_batches:
                    quantise_span(n - 1)
                if 2 <= n <= n_batches + 1:
                    multiply_span(n - 2)
                if n >= 3:
                    add_bias(n - 3)

            for first_c in range(0, CH, X_PIECE):
                chans = slice(first_c, first_c + X_PIECE)
                nc.sync.dma_start(out=x_group[:, chans, :], in_=x_by_group[:, chans, :])

        end_band = BAND_FIRST + BAND_PIX
        first_tail = PIX - BLOCK_PIX
        n_band_quads = (BAND_PIX + QUAD - 1) // QUAD

        def find_top(first_pix, end_pix):
            part = slice(first_pix, end_pix)
            nc.vector.tensor_reduce(out=top[:, part], in_=weights[:, part, 0:TAPS], axis=AXIS.X, op=ALU.max)
            nc.vector.tensor_scalar(out=top[:, part], in0=top[:, part], scalar1=-1.0, scalar2=None, op0=ALU.mult)

        def exponentials(pix):
            logits = weights[:, pix, 0:TAPS]
            nc.scalar.activation(
                out=logits, in_=logits, func=ACT.Exp, bias=top[:, pix : pix + 1], scale=1.0, accum_out=total[:, pix : pix + 1]
            )

        def normalise(first_pix, end_pix):
            part = slice(first_pix, end_pix)
            nc.vector.reciprocal(out=total[:, part], in_=total[:, part])
            nc.vector.tensor_tensor(
                out=weights[:, part, 0:TAPS],
                in0=weights[:, part, 0:TAPS],
                in1=total[:, part].unsqueeze(2).to_broadcast([P, end_pix - first_pix, TAPS]),
                op=ALU.mult,
            )

        with tc.tile_pool(name="band", bufs=1) as bands, tc.tile_pool(name="mid", bufs=2) as mid, tc.psum_pool(
            name="flip2", bufs=2
        ) as flip2, tc.psum_pool(name="xflip", bufs=2) as xflip, tc.psum_pool(name="osum", bufs=2) as osum, tc.psum_pool(
            name="quads", bufs=2
        ) as quads, tc.tile_pool(name="prods", bufs=6) as prods, tc.tile_pool(name="res", bufs=1) as ress, tc.manual_schedule():
            spread = bands.tile([P, BAND_PIX, PIX], F32, tag="wide")
            nc.gpsimd.memset(spread[:], 0.0)
            spread_hw = spread[:].rearrange("p m (h w) -> p m h w", w=W)
            band = bands.tile([P, G, BAND_PITCH], F32)
            spread_flip = {}

            def spread_weights(m):
                pix = BAND_FIRST + m
                h, w = pix // W, pix % W
                first_j, end_j = max(0, PAD - w), min(KS, W + PAD - w)
                end_i = min(KS, H + PAD - h)
                nc.vector.tensor_scalar(
                    out=spread_hw[:, m, h - PAD : h - PAD + end_i, w + first_j - PAD : w + end_j - PAD],
                    in0=weights[:, pix, 0:TAPS].rearrange("p (i j) -> p i j", j=KS)[:, 0:end_i, first_j:end_j],
                    scalar1=total[:, pix : pix + 1],
                    scalar2=None,
                    op0=ALU.mult,
                )

            def flip_spread(quad):
                spread_flip[quad] = flip2.tile([P, QUAD, G], F32, name="spread_flip")
                for k in range(min(QUAD, BAND_PIX - quad * QUAD)):
                    nc.tensor.transpose(spread_flip[quad][:, k, :], spread[:, quad * QUAD + k, :], ident[:])

            def copy_band(quad):
                n_pix = min(QUAD, BAND_PIX - quad * QUAD)
                copy_out = nc.vector.tensor_copy if quad % 2 else nc.scalar.copy
                copy_out(
                    out=band[:, :, quad * QUAD : quad * QUAD + n_pix],
                    in_=spread_flip[quad][:, 0:n_pix, :].rearrange("p k g -> p g k"),
                )

            n_rounds = (G + GROUPS_PER_ROUND - 1) // GROUPS_PER_ROUND
            x_chan = {}
            x_flip = {}
            x_source = {}
            mid_sums = {}
            head_res = ress.tile([P, G, BLOCK_PIX], F32)
            tail_res = ress.tile([P, LATE_FIRST, BLOCK_PIX], F32)
            late_res = []

            def groups_of(rnd):
                return slice(rnd * GROUPS_PER_ROUND, min(G, (rnd + 1) * GROUPS_PER_ROUND))

            def n_groups_of(rnd):
                return min(GROUPS_PER_ROUND, G - rnd * GROUPS_PER_ROUND)

            def load_chan(rnd):
                x_chan[rnd] = mid.tile([P, GROUPS_PER_ROUND, PIX], BF16, name="x_chan")
                nc.sync.dma_start(out=x_chan[rnd][:, 0 : n_groups_of(rnd), :], in_=x_by_channel[:, groups_of(rnd), :])

            def load_late():
                x_late = keep.tile([P, G - LATE_FIRST, PIX], BF16, tag="x_late")
                nc.sync.dma_start(out=x_late[:], in_=x_by_channel[:, LATE_FIRST:G, :])
                for rnd in range(LATE_FIRST // GROUPS_PER_ROUND, n_rounds):
                    x_chan[rnd] = x_late[:, rnd * GROUPS_PER_ROUND - LATE_FIRST : groups_of(rnd).stop - LATE_FIRST, :]

            def flip_chan(group):
                rnd, k = group // GROUPS_PER_ROUND, group % GROUPS_PER_ROUND
                if k == 0:
                    x_flip[rnd] = xflip.tile([P, GROUPS_PER_ROUND, CH], BF16, name="x_flip")
                nc.tensor.transpose(x_flip[rnd][:, k, :], x_chan[rnd][:, k, :], ident_bf[:])
                if k == GROUPS_PER_ROUND - 1 and (rnd + 2) * GROUPS_PER_ROUND < LATE_FIRST:
                    load_chan(rnd + 2)

            def copy_source(rnd):
                x_source[rnd] = mid.tile([P, GROUPS_PER_ROUND, CH], F32, name="x_source")
                copy_out = nc.vector.tensor_copy if rnd % 2 and rnd > LATE_FIRST // GROUPS_PER_ROUND else nc.scalar.copy
                copy_out(out=x_source[rnd][:, 0 : n_groups_of(rnd), :], in_=x_flip[rnd][:, 0 : n_groups_of(rnd), :])

            def multiply_band(group):
                rnd, k = group // GROUPS_PER_ROUND, group % GROUPS_PER_ROUND
                if k == 0:
                    mid_sums[rnd] = osum.tile([P, GROUPS_PER_ROUND, BAND_PIX], F32, name="mid_sums")
                nc.tensor.matmul(
                    out=mid_sums[rnd][:, k, :],
                    lhsT=x_source[rnd][:, k, :],
                    rhs=band[:, group, 0:BAND_PIX],
                    start=True,
                    stop=True,
                )

            def store_band(rnd):
                n_groups = n_groups_of(rnd)
                sums_of = mid_sums[rnd][:, 0:n_groups, :]
                mid_res = mid.tile([P, GROUPS_PER_ROUND, BAND_STORE], F32)
                nc.scalar.copy(out=mid_res[:, 0:n_groups, :], in_=sums_of[:, :, 0:BAND_STORE])
                nc.scalar.copy(out=tail_res[:, groups_of(rnd), 0 : end_band - first_tail], in_=sums_of[:, :, BAND_STORE:BAND_PIX])
                nc.sync.dma_start(
                    out=out_by_channel[:, groups_of(rnd), BAND_FIRST : BAND_FIRST + BAND_STORE], in_=mid_res[:, 0:n_groups, :]
                )

            def store_late(rnd):
                groups = groups_of(rnd)
                mine = late_res[0][:, groups.start - LATE_FIRST : groups.stop - LATE_FIRST, :]
                copy_out = nc.vector.tensor_copy if rnd % 2 else nc.scalar.copy
                copy_out(out=mine[:, :, 0:BAND_PIX], in_=mid_sums[rnd][:, 0 : n_groups_of(rnd), :])
                nc.sync.dma_start(out=out_by_channel[:, groups, BAND_FIRST:PIX], in_=mine)

            units = []
            for pix in list(range(BAND_FIRST)) + list(range(end_band, PIX)):
                h, w = pix // W, pix % W
                terms = []
                for tap in range(TAPS):
                    source_h, source_w = h + tap // KS - PAD, w + tap % KS - PAD
                    if 0 <= source_h < H and 0 <= source_w < W:
                        terms.append((tap, source_h * W + source_w))
                n_units = (len(terms) + UNIT_TERMS - 1) // UNIT_TERMS
                for u in range(n_units):
                    part = terms[u * len(terms) // n_units : (u + 1) * len(terms) // n_units]
                    units.append((pix, part, u == 0, u == n_units - 1))
            n_units = len(units)
            band_unit = n_band_quads + BAND_LAG + 1
            made = {}
            quad_sums = {}

            split = []
            done_terms = 0
            for u in range(n_units):
                scalar_share, fused_share = EARLY_SHARES if u < band_unit else LATE_SHARES
                n = len(units[u][1])
                n_scalar = int(scalar_share * (done_terms + n)) - int(scalar_share * done_terms)
                n_fused = min(n - n_scalar, int(fused_share * (done_terms + n)) - int(fused_share * done_terms))
                n_fused = min(n_fused, n - n_fused)
                split.append((n_scalar, n - n_scalar - n_fused, n_fused))
                done_terms += n

            most_made = max([split[u][0] + split[u][1] for u in range(n_units)])

            def make_products(u):
                pix, terms = units[u][0], units[u][1]
                n_scalar, n_vector, n_fused = split[u]
                made[u] = prods.tile([P, most_made, CH], F32, name="made")
                for k in range(n_scalar + n_vector):
                    tap, source = terms[k]
                    weight = weights[:, pix, tap : tap + 1]
                    if k < n_scalar:
                        nc.scalar.activation(out=made[u][:, k, :], in_=x_t[:, source, :], func=ACT.Copy, scale=weight)
                    else:
                        nc.vector.tensor_scalar(
                            out=made[u][:, k, :], in0=x_t[:, source, :], scalar1=weight, scalar2=None, op0=ALU.mult
                        )

            def fuse_products(u):
                pix, terms = units[u][0], units[u][1]
                n_scalar, n_vector, n_fused = split[u]
                for k in range(n_fused):
                    tap, source = terms[n_scalar + n_vector + k]
                    mine = made[u][:, k, :]
                    nc.vector.scalar_tensor_tensor(
                        out=mine,
                        in0=x_t[:, source, :],
                        scalar=weights[:, pix, tap : tap + 1],
                        in1=mine,
                        op0=ALU.mult,
                        op1=ALU.add,
                    )

            def sum_products(u):
                pix, first, last = units[u][0], units[u][2], units[u][3]
                n_made = split[u][0] + split[u][1]
                quad = pix // QUAD
                if first and (pix % QUAD == 0 or pix == end_band):
                    quad_sums[quad] = quads.tile([P, QUAD, G], F32, name="quad_sums")
                for k in range(n_made):
                    nc.tensor.matmul(
                        out=quad_sums[quad][:, pix % QUAD, :],
                        lhsT=made[u][:, k, :],
                        rhs=ident[:],
                        is_transpose=True,
                        start=(first and k == 0),
                        stop=(last and k == n_made - 1),
                    )

            def finish_quad(quad):
                first_k = end_band % QUAD if quad == end_band // QUAD else 0
                sums_of = quad_sums[quad][:, first_k:QUAD, :].rearrange("p k g -> p g k")
                pixels = [quad * QUAD + first_k, (quad + 1) * QUAD]
                if pixels[0] < BLOCK_PIX:
                    nc.scalar.copy(out=head_res[:, :, pixels[0] : pixels[1]], in_=sums_of)
                else:
                    if not late_res:
                        late_res.append(bands.tile([P, G - LATE_FIRST, PIX - BAND_FIRST], F32, name="late_res", tag="wide"))
                    nc.scalar.copy(
                        out=tail_res[:, :, pixels[0] - first_tail : pixels[1] - first_tail], in_=sums_of[:, 0:LATE_FIRST, :]
                    )
                    nc.scalar.copy(
                        out=late_res[0][:, :, pixels[0] - BAND_FIRST : pixels[1] - BAND_FIRST], in_=sums_of[:, LATE_FIRST:G, :]
                    )

            def store_block(res, first_pix, groups):
                nc.sync.dma_start(out=out_by_channel[:, groups, first_pix : first_pix + BLOCK_PIX], in_=res[:, groups, :])

            n_pieces = CH // X_PIECE
            find_top(0, BAND_FIRST)
            for pix in range(BAND_FIRST):
                exponentials(pix)
            find_top(BAND_FIRST, end_band)
            for pix in range(BAND_FIRST, end_band):
                exponentials(pix)
            normalise(0, BAND_FIRST)
            for piece in range(n_pieces):
                gather_channels(nc.vector.tensor_copy, 0, BLOCK_PIX // W + PAD, piece)
            find_top(end_band, PIX)
            nc.vector.reciprocal(out=total[:, BAND_FIRST:end_band], in_=total[:, BAND_FIRST:end_band])
            load_chan(0)
            load_chan(1)
            group = 0
            head_done = -1

            def band_step(group):
                if group + FLIP_LEAD < G:
                    flip_chan(group + FLIP_LEAD)
                if (group + 2) % GROUPS_PER_ROUND == 0 and group + 2 < G:
                    copy_source((group + 2) // GROUPS_PER_ROUND)
                multiply_band(group)
                rnd = group // GROUPS_PER_ROUND - 1
                if group % GROUPS_PER_ROUND == STORE_LAG and rnd >= 0:
                    if rnd * GROUPS_PER_ROUND < LATE_FIRST:
                        store_band(rnd)
                    else:
                        store_late(rnd)

            for u in range(n_units + 1):
                if u < n_units:
                    make_products(u)
                if u < n_band_quads:
                    for m in range(u * QUAD, min(BAND_PIX, (u + 1) * QUAD)):
                        spread_weights(m)
                    flip_spread(u)
                if BAND_LAG <= u < n_band_quads + BAND_LAG:
                    copy_band(u - BAND_LAG)
                if u == n_band_quads:
                    for k in range(FLIP_LEAD):
                        flip_chan(k)
                if u == band_unit - 1:
                    copy_source(0)
                if u % TAIL_GATHER_STEP == 0 and u // TAIL_GATHER_STEP <= n_pieces and u:
                    gather_channels(nc.scalar.copy, first_tail // W - PAD, H, u // TAIL_GATHER_STEP - 1)
                if u == TAIL_GATHER_STEP * n_pieces + 2:
                    load_late()
                pix = end_band + (u - band_unit) // TAIL_EXP_STEP
                if end_band <= pix < PIX and (u - band_unit) % TAIL_EXP_STEP == 0:
                    exponentials(pix)
                if pix == PIX and (u - band_unit) % TAIL_EXP_STEP == 1:
                    normalise(end_band, PIX)
                if u >= 1:
                    fuse_products(u - 1)
                    sum_products(u - 1)
                    while group < LATE_FIRST and group * (n_units - band_unit) < (u - band_unit) * LATE_FIRST:
                        band_step(group)
                        group += 1
                done = u - FINISH_DELAY
                if done >= 0 and units[done][3] and units[done][0] % QUAD == QUAD - 1:
                    finish_quad(units[done][0] // QUAD)
                    if units[done][0] == BLOCK_PIX - 1:
                        head_done = u
                if head_done >= 0 and (u - head_done) % HEAD_STORE_STEP == 0 and (u - head_done) // HEAD_STORE_STEP < G // RES_GROUPS:
                    first_g = (u - head_done) // HEAD_STORE_STEP * RES_GROUPS
                    store_block(head_res, 0, slice(first_g, first_g + RES_GROUPS))
            finish_quad(PIX // QUAD - 1)
            for group in range(LATE_FIRST, G):
                band_step(group)
                if group == LATE_FIRST + STORE_LAG:
                    for first_g in range(0, LATE_FIRST, GROUPS_PER_ROUND * 3):
                        store_block(tail_res, first_tail, slice(first_g, first_g + GROUPS_PER_ROUND * 3))
            for rnd in range(n_rounds - 2, n_rounds):
                store_late(rnd)
